import numpy as np
import ml_dtypes


def mxq(x, axis, fmt="e4m3"):
    dtype, down = {"e4m3": (ml_dtypes.float8_e4m3fn, 7), "e5m2": (ml_dtypes.float8_e5m2, 14)}[fmt]
    v = np.moveaxis(np.asarray(x, np.float32).astype(ml_dtypes.bfloat16).astype(np.float64), axis, -1)
    blocks = v.reshape(v.shape[:-1] + (-1, 32))
    amax = np.abs(blocks).max(-1, keepdims=True)
    byte = np.maximum(np.where(amax > 0, np.frexp(amax)[1] - 1 + 127, 0) - down, 1)
    scale = np.exp2(byte - 127.0)
    codes = (blocks / scale).astype(np.float32).astype(dtype).astype(np.float64)
    return np.moveaxis((codes * scale).reshape(v.shape), -1, axis)


WIDE = False


def mx_kscale(k):
    if not WIDE:
        return np.ones(k)
    levels = np.array([10, -10, 5, -5, 0])
    a = np.random.permutation(np.resize(levels, k // 512 * 4)).reshape(k // 512, 4)
    idx = np.arange(k)
    return np.exp2(a[idx // 512, idx % 128 // 32])


BF16 = ml_dtypes.bfloat16


def bf(x):
    return np.asarray(x, np.float32).astype(BF16)


def f64(x):
    return np.asarray(x).astype(np.float64)


B, S, D, H, KVH, HD = 1, 128, 512, 16, 4, 128
THETA = 10000.0


def rope(a, cos, sin):
    a1, a2 = a[..., 0::2], a[..., 1::2]
    c, s = cos[None, None], sin[None, None]
    return np.stack([a1 * c - a2 * s, a1 * s + a2 * c], axis=-1).reshape(a.shape)


def setup_inputs():
    s = mx_kscale(D)
    pos = np.arange(S) + np.random.randint(0, S)
    ang = np.outer(pos, 1.0 / THETA ** (np.arange(0, HD, 2) / HD))
    return {"x": bf(np.random.standard_normal((B, S, D)) * s),
            "cos": bf(np.cos(ang)), "sin": bf(np.sin(ang)),
            "Wq": bf(np.random.standard_normal((D, H * HD)) * 1.5 / np.sqrt(D) / s[:, None]),
            "Wkv": bf(np.random.standard_normal((D, 2 * KVH * HD)) * 1.5 / np.sqrt(D) / s[:, None])}


def reference(x, cos, sin, Wq, Wkv):
    xq = mxq(f64(x), 2, "e4m3")
    q = (xq @ mxq(f64(Wq), 0, "e4m3")).reshape(B, S, H, HD).transpose(0, 2, 1, 3)
    kv = (xq @ mxq(f64(Wkv), 0, "e4m3")).reshape(B, S, 2, KVH, HD)
    k = kv[:, :, 0].transpose(0, 2, 1, 3)
    v = kv[:, :, 1].transpose(0, 2, 1, 3)
    return rope(q, f64(cos), f64(sin)), rope(k, f64(cos), f64(sin)), v

@@ -1,0 +1,145 @@
+from contextlib import ExitStack
+
+import concourse.mybir as mybir
+from concourse.masks import make_identity
+
+BF16 = mybir.dt.bfloat16
+F32 = mybir.dt.float32
+U32 = mybir.dt.uint32
+U8 = mybir.dt.uint8
+FP8X4 = mybir.dt.float8_e4m3fn_x4
+MULT = mybir.AluOpType.mult
+ADD = mybir.AluOpType.add
+
+P = 128
+PACK = 4
+SEQ = 128
+DIM = P * PACK
+HEAD = 128
+PAIRS = HEAD // 2
+Q_HEADS = 16
+KV_HEADS = 4
+GROUP = 4
+CHUNK = GROUP * HEAD
+
+FLOPS = 2 * SEQ * DIM * (Q_HEADS + 2 * KV_HEADS) * HEAD
+
+
+def tile_gqa_pa_s_kernel(tc, x, cos, sin, Wq, Wkv, out_0, out_1, out_2):
+    nc = tc.nc
+
+    chunks = []
+    for g in range(Q_HEADS // GROUP):
+        chunks.append((Wq[:, g * CHUNK : (g + 1) * CHUNK], out_0[0, g * GROUP : (g + 1) * GROUP], True))
+    chunks.append((Wkv[:, 0:CHUNK], out_1[0], True))
+    chunks.append((Wkv[:, CHUNK : 2 * CHUNK], out_2[0], False))
+    n_chunks = len(chunks)
+
+    with ExitStack() as ctx:
+        const = ctx.enter_context(tc.tile_pool(name="const", bufs=1))
+        weights = ctx.enter_context(tc.tile_pool(name="weights", bufs=n_chunks))
+        work = ctx.enter_context(tc.tile_pool(name="work", bufs=n_chunks))
+        psum_x = ctx.enter_context(tc.psum_pool(name="psum_x", bufs=1))
+        psum = ctx.enter_context(tc.psum_pool(name="psum", bufs=n_chunks))
+
+        x_sb = const.tile([SEQ, DIM], BF16)
+        nc.sync.dma_start(out=x_sb[:], in_=x[0])
+        cos_sb = const.tile([SEQ, PAIRS], BF16)
+        nc.scalar.dma_start(out=cos_sb[:], in_=cos)
+        sin_sb = const.tile([SEQ, PAIRS], BF16)
+        nc.scalar.dma_start(out=sin_sb[:], in_=sin)
+        raws = []
+        for w_cols, heads_out, rotated in chunks:
+            raw = weights.tile([P, PACK, CHUNK], BF16)
+            nc.sync.dma_start(out=raw[:], in_=w_cols.rearrange("(p t) w -> p t w", t=PACK))
+            raws.append(raw)
+
+        ident = const.tile([P, P], F32)
+        make_identity(nc, ident[:])
+        x_words = x_sb[:].bitcast(F32).rearrange("s (p u) -> s u p", u=2)
+        x_t = psum_x.tile([P, 2, SEQ], F32)
+        for u in range(2):
+            nc.tensor.transpose(x_t[:, u, :], x_words[:, u, :], ident[:])
+        x_grouped = const.tile([P, SEQ * PACK], BF16, align_bytes=64)
+        nc.vector.tensor_copy(
+            out=x_grouped[:].bitcast(F32).rearrange("p (s u) -> p s u", u=2),
+            in_=x_t[:].rearrange("p u s -> p s u"),
+        )
+        x_codes = const.tile([P, SEQ], U32, align_bytes=64)
+        x_scales = const.tile([P, SEQ], U8, align_bytes=64)
+        nc.vector.quantize_mx(out=x_codes[:].bitcast(FP8X4), scales=x_scales[:], in_=x_grouped[:])
+
+        neg_sin = const.tile([SEQ, PAIRS], BF16)
+        nc.scalar.mul(out=neg_sin[:], in_=sin_sb[:], mul=-1.0)
+
+        def project(c):
+            grouped = weights.tile([P, CHUNK, PACK], BF16, align_bytes=64)
+            dst = grouped[:].rearrange("p (c i) t -> p c t i", i=4)
+            src = raws[c][:].rearrange("p t (c i) -> p c t i", i=4)
+            if c == 0:
+                nc.vector.tensor_copy(out=dst, in_=src)
+            else:
+                nc.scalar.copy(out=dst, in_=src)
+            codes = weights.tile([P, CHUNK], U32, align_bytes=64)
+            scales = weights.tile([P, CHUNK], U8, align_bytes=64)
+            nc.vector.quantize_mx(
+                out=codes[:].bitcast(FP8X4),
+                scales=scales[:],
+                in_=grouped[:].rearrange("p w t -> p (w t)"),
+            )
+            acc = psum.tile([SEQ, CHUNK], F32)
+            nc.tensor.matmul_mx(
+                out=acc[:],
+                lhsT=x_codes[:].bitcast(FP8X4),
+                lhsT_scale=x_scales[:],
+                rhs=codes[:].bitcast(FP8X4),
+                rhs_scale=scales[:],
+                start=True,
+                stop=True,
+            )
+            return acc
+
+        def finish(c, acc):
+            heads_out = chunks[c][1]
+            result = work.tile([SEQ, CHUNK], F32)
+            if chunks[c][2]:
+                lanes = acc[:].rearrange("p (h i e) -> p h i e", h=GROUP, e=2)
+                straight = work.tile([SEQ, CHUNK], F32)
+                nc.vector.tensor_tensor(
+                    out=straight[:].rearrange("p (h i e) -> p h i e", h=GROUP, e=2),
+                    in0=lanes,
+                    in1=cos_sb[:].unsqueeze(1).unsqueeze(3).to_broadcast([SEQ, GROUP, PAIRS, 2]),
+                    op=MULT,
+                )
+                crossed = work.tile([SEQ, 2, GROUP * PAIRS], F32)
+                nc.vector.tensor_tensor(
+                    out=crossed[:, 0, :].rearrange("p (h i) -> p h i", h=GROUP),
+                    in0=lanes[:, :, :, 1],
+                    in1=neg_sin[:].unsqueeze(1).to_broadcast([SEQ, GROUP, PAIRS]),
+                    op=MULT,
+                )
+                nc.vector.tensor_tensor(
+                    out=crossed[:, 1, :].rearrange("p (h i) -> p h i", h=GROUP),
+                    in0=lanes[:, :, :, 0],
+                    in1=sin_sb[:].unsqueeze(1).to_broadcast([SEQ, GROUP, PAIRS]),
+                    op=MULT,
+                )
+                nc.vector.tensor_tensor(
+                    out=result[:].rearrange("p (n e) -> p n e", e=2),
+                    in0=straight[:].rearrange("p (n e) -> p n e", e=2),
+                    in1=crossed[:].rearrange("p e n -> p n e"),
+                    op=ADD,
+                )
+            else:
+                nc.scalar.copy(out=result[:], in_=acc[:])
+            nc.sync.dma_start(
+                out=heads_out.rearrange("h s d -> s h d"),
+                in_=result[:].rearrange("p (h d) -> p h d", h=GROUP),
+            )
+
+        banks = []
+        for c in range(n_chunks):
+            banks.append(project(c))
+            if c >= 1:
+                finish(c - 1, banks[c - 1])
+        finish(n_chunks - 1, banks[n_chunks - 1])

@@ -21,6 +21,9 @@ Q_HEADS = 16
 KV_HEADS = 4
 GROUP = 4
 CHUNK = GROUP * HEAD
+RUN = 4
+
+VECTOR_COLS = (336, 336, 0, 0, 0, 0)
 
 FLOPS = 2 * SEQ * DIM * (Q_HEADS + 2 * KV_HEADS) * HEAD
 
@@ -41,6 +44,7 @@ def tile_gqa_pa_s_kernel(tc, x, cos, sin, Wq, Wkv, out_0, out_1, out_2):
         work = ctx.enter_context(tc.tile_pool(name="work", bufs=n_chunks))
         psum_x = ctx.enter_context(tc.psum_pool(name="psum_x", bufs=1))
         psum = ctx.enter_context(tc.psum_pool(name="psum", bufs=n_chunks))
+        ctx.enter_context(tc.manual_schedule())
 
         x_sb = const.tile([SEQ, DIM], BF16)
         nc.sync.dma_start(out=x_sb[:], in_=x[0])
@@ -49,10 +53,18 @@ def tile_gqa_pa_s_kernel(tc, x, cos, sin, Wq, Wkv, out_0, out_1, out_2):
         sin_sb = const.tile([SEQ, PAIRS], BF16)
         nc.scalar.dma_start(out=sin_sb[:], in_=sin)
         raws = []
-        for w_cols, heads_out, rotated in chunks:
+        for c in range(n_chunks):
+            rows = chunks[c][0].rearrange("(p t) w -> p t w", t=PACK)
             raw = weights.tile([P, PACK, CHUNK], BF16)
-            nc.sync.dma_start(out=raw[:], in_=w_cols.rearrange("(p t) w -> p t w", t=PACK))
+            cut = VECTOR_COLS[c] if c == 0 else 0
+            if cut:
+                nc.sync.dma_start(out=raw[:, :, 0:cut], in_=rows[:, :, 0:cut])
+            nc.sync.dma_start(out=raw[:, :, cut:CHUNK], in_=rows[:, :, cut:CHUNK])
             raws.append(raw)
+
+        warm = const.tile([P, 2], F32)
+        nc.vector.memset(warm[:], 0.0)
+        nc.scalar.copy(out=warm[:, 1:2], in_=warm[:, 0:1])
 
         ident = const.tile([P, P], F32)
         make_identity(nc, ident[:])
@@ -60,32 +72,41 @@ def tile_gqa_pa_s_kernel(tc, x, cos, sin, Wq, Wkv, out_0, out_1, out_2):
         x_t = psum_x.tile([P, 2, SEQ], F32)
         for u in range(2):
             nc.tensor.transpose(x_t[:, u, :], x_words[:, u, :], ident[:])
-        x_grouped = const.tile([P, SEQ * PACK], BF16, align_bytes=64)
-        nc.vector.tensor_copy(
-            out=x_grouped[:].bitcast(F32).rearrange("p (s u) -> p s u", u=2),
-            in_=x_t[:].rearrange("p u s -> p s u"),
-        )
+
+        factors = const.tile([SEQ, 2, PAIRS, 2], BF16)
+        nc.scalar.copy(out=factors[:, 0, :, :], in_=cos_sb[:].unsqueeze(2).to_broadcast([SEQ, PAIRS, 2]))
+        nc.scalar.copy(out=factors[:, 1, :, 0], in_=sin_sb[:])
+        nc.scalar.mul(out=factors[:, 1, :, 1], in_=sin_sb[:], mul=-1.0)
+
+        groupeds = []
+        for c in range(n_chunks):
+            grouped = weights.tile([P, CHUNK, PACK], BF16, align_bytes=64)
+            groupeds.append(grouped)
+
+        def regroup(copy, c, lo, hi):
+            if hi > lo:
+                copy(
+                    out=groupeds[c][:, lo:hi, :].rearrange("p (c i) t -> p c t i", i=RUN),
+                    in_=raws[c][:, :, lo:hi].rearrange("p t (c i) -> p c t i", i=RUN),
+                )
+
+        def regroup_vector(c):
+            regroup(nc.vector.tensor_copy, c, 0, VECTOR_COLS[c])
+
+        def regroup_scalar(c):
+            regroup(nc.scalar.copy, c, VECTOR_COLS[c], CHUNK)
+
         x_codes = const.tile([P, SEQ], U32, align_bytes=64)
         x_scales = const.tile([P, SEQ], U8, align_bytes=64)
-        nc.vector.quantize_mx(out=x_codes[:].bitcast(FP8X4), scales=x_scales[:], in_=x_grouped[:])
-
-        neg_sin = const.tile([SEQ, PAIRS], BF16)
-        nc.scalar.mul(out=neg_sin[:], in_=sin_sb[:], mul=-1.0)
+        banks = {}
 
         def project(c):
-            grouped = weights.tile([P, CHUNK, PACK], BF16, align_bytes=64)
-            dst = grouped[:].rearrange("p (c i) t -> p c t i", i=4)
-            src = raws[c][:].rearrange("p t (c i) -> p c t i", i=4)
-            if c == 0:
-                nc.vector.tensor_copy(out=dst, in_=src)
-            else:
-                nc.scalar.copy(out=dst, in_=src)
             codes = weights.tile([P, CHUNK], U32, align_bytes=64)
             scales = weights.tile([P, CHUNK], U8, align_bytes=64)
             nc.vector.quantize_mx(
                 out=codes[:].bitcast(FP8X4),
                 scales=scales[:],
-                in_=grouped[:].rearrange("p w t -> p (w t)"),
+                in_=groupeds[c][:].rearrange("p w t -> p (w t)"),
             )
             acc = psum.tile([SEQ, CHUNK], F32)
             nc.tensor.matmul_mx(
@@ -97,49 +118,59 @@ def tile_gqa_pa_s_kernel(tc, x, cos, sin, Wq, Wkv, out_0, out_1, out_2):
                 start=True,
                 stop=True,
             )
-            return acc
+            banks[c] = acc
 
-        def finish(c, acc):
-            heads_out = chunks[c][1]
-            result = work.tile([SEQ, CHUNK], F32)
-            if chunks[c][2]:
-                lanes = acc[:].rearrange("p (h i e) -> p h i e", h=GROUP, e=2)
-                straight = work.tile([SEQ, CHUNK], F32)
-                nc.vector.tensor_tensor(
-                    out=straight[:].rearrange("p (h i e) -> p h i e", h=GROUP, e=2),
-                    in0=lanes,
-                    in1=cos_sb[:].unsqueeze(1).unsqueeze(3).to_broadcast([SEQ, GROUP, PAIRS, 2]),
-                    op=MULT,
-                )
-                crossed = work.tile([SEQ, 2, GROUP * PAIRS], F32)
-                nc.vector.tensor_tensor(
-                    out=crossed[:, 0, :].rearrange("p (h i) -> p h i", h=GROUP),
-                    in0=lanes[:, :, :, 1],
-                    in1=neg_sin[:].unsqueeze(1).to_broadcast([SEQ, GROUP, PAIRS]),
-                    op=MULT,
-                )
-                nc.vector.tensor_tensor(
-                    out=crossed[:, 1, :].rearrange("p (h i) -> p h i", h=GROUP),
-                    in0=lanes[:, :, :, 0],
-                    in1=sin_sb[:].unsqueeze(1).to_broadcast([SEQ, GROUP, PAIRS]),
-                    op=MULT,
-                )
-                nc.vector.tensor_tensor(
-                    out=result[:].rearrange("p (n e) -> p n e", e=2),
-                    in0=straight[:].rearrange("p (n e) -> p n e", e=2),
-                    in1=crossed[:].rearrange("p e n -> p n e"),
-                    op=ADD,
-                )
-            else:
-                nc.scalar.copy(out=result[:], in_=acc[:])
+        products = {}
+
+        def multiply(c):
+            product = work.tile([SEQ, 2, CHUNK], F32)
+            nc.vector.tensor_tensor(
+                out=product[:].rearrange("p j (h d) -> p j h d", h=GROUP),
+                in0=banks[c][:].rearrange("p (h d) -> p h d", h=GROUP).unsqueeze(1).to_broadcast([SEQ, 2, GROUP, HEAD]),
+                in1=factors[:].rearrange("p j i e -> p j (i e)").unsqueeze(2).to_broadcast([SEQ, 2, GROUP, HEAD]),
+                op=MULT,
+            )
+            products[c] = product
+
+        def store(c, result):
             nc.sync.dma_start(
-                out=heads_out.rearrange("h s d -> s h d"),
+                out=chunks[c][1].rearrange("h s d -> s h d"),
                 in_=result[:].rearrange("p (h d) -> p h d", h=GROUP),
             )
 
-        banks = []
-        for c in range(n_chunks):
-            banks.append(project(c))
-            if c >= 1:
-                finish(c - 1, banks[c - 1])
-        finish(n_chunks - 1, banks[n_chunks - 1])
+        def combine(c):
+            result = work.tile([SEQ, CHUNK], F32)
+            nc.vector.tensor_tensor(
+                out=result[:].rearrange("p (n e) -> p n e", e=2),
+                in0=products[c][:, 0, :].rearrange("p (n e) -> p n e", e=2),
+                in1=products[c][:, 1, :].rearrange("p (n e) -> p n e", e=2)[:, :, ::-1],
+                op=ADD,
+            )
+            store(c, result)
+
+        regroup_vector(0)
+        x_grouped = const.tile([P, SEQ * PACK], BF16, align_bytes=64)
+        nc.scalar.copy(
+            out=x_grouped[:].bitcast(F32).rearrange("p (s u) -> p s u", u=2),
+            in_=x_t[:].rearrange("p u s -> p s u"),
+        )
+        regroup_scalar(0)
+        nc.vector.quantize_mx(out=x_codes[:].bitcast(FP8X4), scales=x_scales[:], in_=x_grouped[:])
+        project(0)
+        regroup_vector(1)
+        regroup_scalar(1)
+        regroup_scalar(2)
+        project(1)
+
+        for c in range(n_chunks - 1):
+            if c + 3 < n_chunks:
+                regroup_scalar(c + 3)
+            multiply(c)
+            if c + 2 < n_chunks:
+                project(c + 2)
+            combine(c)
+
+        last = n_chunks - 1
+        values = work.tile([SEQ, CHUNK], F32)
+        nc.scalar.copy(out=values[:], in_=banks[last][:])
+        store(last, values)

@@ -23,7 +23,7 @@ GROUP = 4
 CHUNK = GROUP * HEAD
 RUN = 4
 
-VECTOR_COLS = (336, 336, 0, 0, 0, 0)
+VECTOR_COLS = (336, 336, 96, 96, 96, 96)
 
 FLOPS = 2 * SEQ * DIM * (Q_HEADS + 2 * KV_HEADS) * HEAD
 
@@ -78,10 +78,13 @@ def tile_gqa_pa_s_kernel(tc, x, cos, sin, Wq, Wkv, out_0, out_1, out_2):
         nc.scalar.copy(out=factors[:, 1, :, 0], in_=sin_sb[:])
         nc.scalar.mul(out=factors[:, 1, :, 1], in_=sin_sb[:], mul=-1.0)
 
+        overlay = ctx.enter_context(tc.tile_pool(name="overlay", bufs=1))
+        grouped_bytes = CHUNK * PACK * 2
         groupeds = []
         for c in range(n_chunks):
-            grouped = weights.tile([P, CHUNK, PACK], BF16, align_bytes=64)
-            groupeds.append(grouped)
+            groupeds.append(
+                overlay.tile([P, CHUNK, PACK], BF16, name="grouped%d" % c, offset=c * grouped_bytes, align_bytes=64)
+            )
 
         def regroup(copy, c, lo, hi):
             if hi > lo:
@@ -139,8 +142,13 @@ def tile_gqa_pa_s_kernel(tc, x, cos, sin, Wq, Wkv, out_0, out_1, out_2):
             )
 
         def combine(c):
-            result = work.tile([SEQ, CHUNK], F32)
-            nc.vector.tensor_tensor(
+            if c + 2 < n_chunks:
+                engine = nc.gpsimd
+                result = overlay.tile([SEQ, CHUNK], F32, name="result%d" % c, offset=(c + 2) * grouped_bytes, align_bytes=64)
+            else:
+                engine = nc.vector
+                result = work.tile([SEQ, CHUNK], F32, name="result_last")
+            engine.tensor_tensor(
                 out=result[:].rearrange("p (n e) -> p n e", e=2),
                 in0=products[c][:, 0, :].rearrange("p (n e) -> p n e", e=2),
                 in1=products[c][:, 1, :].rearrange("p (n e) -> p n e", e=2)[:, :, ::-1],
@@ -159,13 +167,15 @@ def tile_gqa_pa_s_kernel(tc, x, cos, sin, Wq, Wkv, out_0, out_1, out_2):
         project(0)
         regroup_vector(1)
         regroup_scalar(1)
+        regroup_vector(2)
         regroup_scalar(2)
         project(1)
 
         for c in range(n_chunks - 1):
-            if c + 3 < n_chunks:
-                regroup_scalar(c + 3)
             multiply(c)
+            if c + 3 < n_chunks:
+                regroup_vector(c + 3)
+                regroup_scalar(c + 3)
             if c + 2 < n_chunks:
                 project(c + 2)
             combine(c)

@@ -23,7 +23,8 @@ GROUP = 4
 CHUNK = GROUP * HEAD
 RUN = 4
 
-VECTOR_COLS = (336, 336, 96, 96, 96, 96)
+VECTOR_COLS = (336, 336, 64, 64, 64, 64)
+GPSIMD_HEADS = 3
 
 FLOPS = 2 * SEQ * DIM * (Q_HEADS + 2 * KV_HEADS) * HEAD
 
@@ -135,26 +136,29 @@ def tile_gqa_pa_s_kernel(tc, x, cos, sin, Wq, Wkv, out_0, out_1, out_2):
             )
             products[c] = product
 
-        def store(c, result):
-            nc.sync.dma_start(
-                out=chunks[c][1].rearrange("h s d -> s h d"),
-                in_=result[:].rearrange("p (h d) -> p h d", h=GROUP),
-            )
-
-        def combine(c):
-            if c + 2 < n_chunks:
-                engine = nc.gpsimd
-                result = overlay.tile([SEQ, CHUNK], F32, name="result%d" % c, offset=(c + 2) * grouped_bytes, align_bytes=64)
-            else:
-                engine = nc.vector
-                result = work.tile([SEQ, CHUNK], F32, name="result_last")
+        def add_and_store(engine, c, result, first, heads):
+            lanes = slice(first * HEAD, (first + heads) * HEAD)
             engine.tensor_tensor(
                 out=result[:].rearrange("p (n e) -> p n e", e=2),
-                in0=products[c][:, 0, :].rearrange("p (n e) -> p n e", e=2),
-                in1=products[c][:, 1, :].rearrange("p (n e) -> p n e", e=2)[:, :, ::-1],
+                in0=products[c][:, 0, lanes].rearrange("p (n e) -> p n e", e=2),
+                in1=products[c][:, 1, lanes].rearrange("p (n e) -> p n e", e=2)[:, :, ::-1],
                 op=ADD,
             )
-            store(c, result)
+            nc.sync.dma_start(
+                out=chunks[c][1][first : first + heads].rearrange("h s d -> s h d"),
+                in_=result[:].rearrange("p (h d) -> p h d", h=heads),
+            )
+
+        def combine_vector(c, first):
+            heads = GROUP - first
+            result_v = work.tile([SEQ, heads * HEAD], F32)
+            add_and_store(nc.vector, c, result_v, first, heads)
+
+        def combine_gpsimd(c):
+            result_g = overlay.tile(
+                [SEQ, GPSIMD_HEADS * HEAD], F32, name="result%d" % c, offset=(c + 2) * grouped_bytes, align_bytes=64
+            )
+            add_and_store(nc.gpsimd, c, result_g, 0, GPSIMD_HEADS)
 
         regroup_vector(0)
         x_grouped = const.tile([P, SEQ * PACK], BF16, align_bytes=64)
@@ -177,10 +181,16 @@ def tile_gqa_pa_s_kernel(tc, x, cos, sin, Wq, Wkv, out_0, out_1, out_2):
                 regroup_vector(c + 3)
                 regroup_scalar(c + 3)
             if c + 2 < n_chunks:
+                combine_vector(c, GPSIMD_HEADS)
                 project(c + 2)
-            combine(c)
+                combine_gpsimd(c)
+            else:
+                combine_vector(c, 0)
 
         last = n_chunks - 1
         values = work.tile([SEQ, CHUNK], F32)
         nc.scalar.copy(out=values[:], in_=banks[last][:])
-        store(last, values)
+        nc.sync.dma_start(
+            out=chunks[last][1].rearrange("h s d -> s h d"),
+            in_=values[:].rearrange("p (h d) -> p h d", h=GROUP),
+        )

@@ -126,22 +126,25 @@ def tile_gqa_pa_s_kernel(tc, x, cos, sin, Wq, Wkv, out_0, out_1, out_2):
 
         products = {}
 
-        def multiply(c):
-            product = work.tile([SEQ, 2, CHUNK], F32)
+        def multiply(c, first, heads):
+            product = work.tile([SEQ, 2, heads * HEAD], F32)
+            lanes = slice(first * HEAD, (first + heads) * HEAD)
             nc.vector.tensor_tensor(
-                out=product[:].rearrange("p j (h d) -> p j h d", h=GROUP),
-                in0=banks[c][:].rearrange("p (h d) -> p h d", h=GROUP).unsqueeze(1).to_broadcast([SEQ, 2, GROUP, HEAD]),
-                in1=factors[:].rearrange("p j i e -> p j (i e)").unsqueeze(2).to_broadcast([SEQ, 2, GROUP, HEAD]),
+                out=product[:].rearrange("p j (h d) -> p j h d", h=heads),
+                in0=banks[c][:, lanes].rearrange("p (h d) -> p h d", h=heads).unsqueeze(1).to_broadcast([SEQ, 2, heads, HEAD]),
+                in1=factors[:].rearrange("p j i e -> p j (i e)").unsqueeze(2).to_broadcast([SEQ, 2, heads, HEAD]),
                 op=MULT,
             )
-            products[c] = product
+            for h in range(first, first + heads):
+                products[c, h] = (product, h - first)
 
         def add_and_store(engine, c, result, first, heads):
-            lanes = slice(first * HEAD, (first + heads) * HEAD)
+            product, place = products[c, first]
+            lanes = slice(place * HEAD, (place + heads) * HEAD)
             engine.tensor_tensor(
                 out=result[:].rearrange("p (n e) -> p n e", e=2),
-                in0=products[c][:, 0, lanes].rearrange("p (n e) -> p n e", e=2),
-                in1=products[c][:, 1, lanes].rearrange("p (n e) -> p n e", e=2)[:, :, ::-1],
+                in0=product[:, 0, lanes].rearrange("p (n e) -> p n e", e=2),
+                in1=product[:, 1, lanes].rearrange("p (n e) -> p n e", e=2)[:, :, ::-1],
                 op=ADD,
             )
             nc.sync.dma_start(
@@ -149,8 +152,7 @@ def tile_gqa_pa_s_kernel(tc, x, cos, sin, Wq, Wkv, out_0, out_1, out_2):
                 in_=result[:].rearrange("p (h d) -> p h d", h=heads),
             )
 
-        def combine_vector(c, first):
-            heads = GROUP - first
+        def combine_vector(c, first, heads):
             result_v = work.tile([SEQ, heads * HEAD], F32)
             add_and_store(nc.vector, c, result_v, first, heads)
 
@@ -175,17 +177,14 @@ def tile_gqa_pa_s_kernel(tc, x, cos, sin, Wq, Wkv, out_0, out_1, out_2):
         regroup_scalar(2)
         project(1)
 
-        for c in range(n_chunks - 1):
-            multiply(c)
+        for c in range(n_chunks - 2):
+            multiply(c, 0, GROUP)
             if c + 3 < n_chunks:
                 regroup_vector(c + 3)
                 regroup_scalar(c + 3)
-            if c + 2 < n_chunks:
-                combine_vector(c, GPSIMD_HEADS)
-                project(c + 2)
-                combine_gpsimd(c)
-            else:
-                combine_vector(c, 0)
+            combine_vector(c, GPSIMD_HEADS, GROUP - GPSIMD_HEADS)
+            project(c + 2)
+            combine_gpsimd(c)
 
         last = n_chunks - 1
         values = work.tile([SEQ, CHUNK], F32)
@@ -194,3 +193,9 @@ def tile_gqa_pa_s_kernel(tc, x, cos, sin, Wq, Wkv, out_0, out_1, out_2):
             out=chunks[last][1].rearrange("h s d -> s h d"),
             in_=values[:].rearrange("p (h d) -> p h d", h=GROUP),
         )
+
+        half = GROUP // 2
+        multiply(last - 1, 0, half)
+        multiply(last - 1, half, half)
+        combine_vector(last - 1, 0, half)
+        combine_vector(last - 1, half, half)

@@ -23,7 +23,8 @@ GROUP = 4
 CHUNK = GROUP * HEAD
 RUN = 4
 
-VECTOR_COLS = (336, 336, 64, 64, 64, 64)
+VECTOR_COLS = (384, 256, 64, 64, 64, 64)
+FIRST_LOAD = CHUNK // 2
 GPSIMD_HEADS = 3
 
 FLOPS = 2 * SEQ * DIM * (Q_HEADS + 2 * KV_HEADS) * HEAD
@@ -57,7 +58,7 @@ def tile_gqa_pa_s_kernel(tc, x, cos, sin, Wq, Wkv, out_0, out_1, out_2):
         for c in range(n_chunks):
             rows = chunks[c][0].rearrange("(p t) w -> p t w", t=PACK)
             raw = weights.tile([P, PACK, CHUNK], BF16)
-            cut = VECTOR_COLS[c] if c == 0 else 0
+            cut = FIRST_LOAD if c == 0 else 0
             if cut:
                 nc.sync.dma_start(out=raw[:, :, 0:cut], in_=rows[:, :, 0:cut])
             nc.sync.dma_start(out=raw[:, :, cut:CHUNK], in_=rows[:, :, cut:CHUNK])
@@ -95,7 +96,11 @@ def tile_gqa_pa_s_kernel(tc, x, cos, sin, Wq, Wkv, out_0, out_1, out_2):
                 )
 
         def regroup_vector(c):
-            regroup(nc.vector.tensor_copy, c, 0, VECTOR_COLS[c])
+            if c == 0:
+                regroup(nc.vector.tensor_copy, c, 0, FIRST_LOAD)
+                regroup(nc.vector.tensor_copy, c, FIRST_LOAD, VECTOR_COLS[c])
+            else:
+                regroup(nc.vector.tensor_copy, c, 0, VECTOR_COLS[c])
 
         def regroup_scalar(c):
             regroup(nc.scalar.copy, c, VECTOR_COLS[c], CHUNK)

@@ -36,8 +36,8 @@ def tile_gqa_pa_s_kernel(tc, x, cos, sin, Wq, Wkv, out_0, out_1, out_2):
     chunks = []
     for g in range(Q_HEADS // GROUP):
         chunks.append((Wq[:, g * CHUNK : (g + 1) * CHUNK], out_0[0, g * GROUP : (g + 1) * GROUP], True))
-    chunks.append((Wkv[:, 0:CHUNK], out_1[0], True))
     chunks.append((Wkv[:, CHUNK : 2 * CHUNK], out_2[0], False))
+    chunks.append((Wkv[:, 0:CHUNK], out_1[0], True))
     n_chunks = len(chunks)
 
     with ExitStack() as ctx:
@@ -182,25 +182,29 @@ def tile_gqa_pa_s_kernel(tc, x, cos, sin, Wq, Wkv, out_0, out_1, out_2):
         regroup_scalar(2)
         project(1)
 
-        for c in range(n_chunks - 2):
+        for c in range(n_chunks - 3):
             multiply(c, 0, GROUP)
-            if c + 3 < n_chunks:
-                regroup_vector(c + 3)
-                regroup_scalar(c + 3)
+            regroup_vector(c + 3)
+            regroup_scalar(c + 3)
             combine_vector(c, GPSIMD_HEADS, GROUP - GPSIMD_HEADS)
             project(c + 2)
             combine_gpsimd(c)
 
-        last = n_chunks - 1
+        values_at = n_chunks - 2
         values = work.tile([SEQ, CHUNK], F32)
-        nc.scalar.copy(out=values[:], in_=banks[last][:])
+        nc.scalar.copy(out=values[:], in_=banks[values_at][:])
         nc.sync.dma_start(
-            out=chunks[last][1].rearrange("h s d -> s h d"),
+            out=chunks[values_at][1].rearrange("h s d -> s h d"),
             in_=values[:].rearrange("p (h d) -> p h d", h=GROUP),
         )
 
+        last = n_chunks - 1
+        multiply(values_at - 1, 0, GROUP)
+        project(last)
+        combine_vector(values_at - 1, 0, GROUP)
+
         half = GROUP // 2
-        multiply(last - 1, 0, half)
-        multiply(last - 1, half, half)
-        combine_vector(last - 1, 0, half)
-        combine_vector(last - 1, half, half)
+        multiply(last, 0, half)
+        multiply(last, half, half)
+        combine_vector(last, 0, half)
+        combine_vector(last, half, half)

@@ -23,7 +23,7 @@ GROUP = 4
 CHUNK = GROUP * HEAD
 RUN = 4
 
-VECTOR_COLS = (384, 256, 64, 64, 64, 64)
+VECTOR_COLS = (384, 256, 64, 64, 64, 32, 32)
 FIRST_LOAD = CHUNK // 2
 GPSIMD_HEADS = 3
 
@@ -37,13 +37,17 @@ def tile_gqa_pa_s_kernel(tc, x, cos, sin, Wq, Wkv, out_0, out_1, out_2):
     for g in range(Q_HEADS // GROUP):
         chunks.append((Wq[:, g * CHUNK : (g + 1) * CHUNK], out_0[0, g * GROUP : (g + 1) * GROUP], True))
     chunks.append((Wkv[:, CHUNK : 2 * CHUNK], out_2[0], False))
-    chunks.append((Wkv[:, 0:CHUNK], out_1[0], True))
+    half = GROUP // 2
+    for g in range(2):
+        chunks.append((Wkv[:, g * half * HEAD : (g + 1) * half * HEAD], out_1[0, g * half : (g + 1) * half], True))
     n_chunks = len(chunks)
+    widths = [w_cols.shape[1] for w_cols, heads_out, rotated in chunks]
 
     with ExitStack() as ctx:
         const = ctx.enter_context(tc.tile_pool(name="const", bufs=1))
         weights = ctx.enter_context(tc.tile_pool(name="weights", bufs=n_chunks))
         work = ctx.enter_context(tc.tile_pool(name="work", bufs=n_chunks))
+        overlay = ctx.enter_context(tc.tile_pool(name="overlay", bufs=1))
         psum_x = ctx.enter_context(tc.psum_pool(name="psum_x", bufs=1))
         psum = ctx.enter_context(tc.psum_pool(name="psum", bufs=n_chunks))
         ctx.enter_context(tc.manual_schedule())
@@ -57,11 +61,11 @@ def tile_gqa_pa_s_kernel(tc, x, cos, sin, Wq, Wkv, out_0, out_1, out_2):
         raws = []
         for c in range(n_chunks):
             rows = chunks[c][0].rearrange("(p t) w -> p t w", t=PACK)
-            raw = weights.tile([P, PACK, CHUNK], BF16)
+            raw = weights.tile([P, PACK, widths[c]], BF16)
             cut = FIRST_LOAD if c == 0 else 0
             if cut:
                 nc.sync.dma_start(out=raw[:, :, 0:cut], in_=rows[:, :, 0:cut])
-            nc.sync.dma_start(out=raw[:, :, cut:CHUNK], in_=rows[:, :, cut:CHUNK])
+            nc.sync.dma_start(out=raw[:, :, cut : widths[c]], in_=rows[:, :, cut : widths[c]])
             raws.append(raw)
 
         warm = const.tile([P, 2], F32)
@@ -80,20 +84,18 @@ def tile_gqa_pa_s_kernel(tc, x, cos, sin, Wq, Wkv, out_0, out_1, out_2):
         nc.scalar.copy(out=factors[:, 1, :, 0], in_=sin_sb[:])
         nc.scalar.mul(out=factors[:, 1, :, 1], in_=sin_sb[:], mul=-1.0)
 
-        overlay = ctx.enter_context(tc.tile_pool(name="overlay", bufs=1))
-        grouped_bytes = CHUNK * PACK * 2
+        places = [sum(widths[:c]) * PACK * 2 for c in range(n_chunks)]
         groupeds = []
         for c in range(n_chunks):
             groupeds.append(
-                overlay.tile([P, CHUNK, PACK], BF16, name="grouped%d" % c, offset=c * grouped_bytes, align_bytes=64)
+                overlay.tile([P, widths[c], PACK], BF16, name="grouped%d" % c, offset=places[c], align_bytes=64)
             )
 
         def regroup(copy, c, lo, hi):
-            if hi > lo:
-                copy(
-                    out=groupeds[c][:, lo:hi, :].rearrange("p (c i) t -> p c t i", i=RUN),
-                    in_=raws[c][:, :, lo:hi].rearrange("p t (c i) -> p c t i", i=RUN),
-                )
+            copy(
+                out=groupeds[c][:, lo:hi, :].rearrange("p (c i) t -> p c t i", i=RUN),
+                in_=raws[c][:, :, lo:hi].rearrange("p t (c i) -> p c t i", i=RUN),
+            )
 
         def regroup_vector(c):
             if c == 0:
@@ -103,21 +105,21 @@ def tile_gqa_pa_s_kernel(tc, x, cos, sin, Wq, Wkv, out_0, out_1, out_2):
                 regroup(nc.vector.tensor_copy, c, 0, VECTOR_COLS[c])
 
         def regroup_scalar(c):
-            regroup(nc.scalar.copy, c, VECTOR_COLS[c], CHUNK)
+            regroup(nc.scalar.copy, c, VECTOR_COLS[c], widths[c])
 
         x_codes = const.tile([P, SEQ], U32, align_bytes=64)
         x_scales = const.tile([P, SEQ], U8, align_bytes=64)
         banks = {}
 
         def project(c):
-            codes = weights.tile([P, CHUNK], U32, align_bytes=64)
-            scales = weights.tile([P, CHUNK], U8, align_bytes=64)
+            codes = weights.tile([P, widths[c]], U32, align_bytes=64)
+            scales = weights.tile([P, widths[c]], U8, align_bytes=64)
             nc.vector.quantize_mx(
                 out=codes[:].bitcast(FP8X4),
                 scales=scales[:],
                 in_=groupeds[c][:].rearrange("p w t -> p (w t)"),
             )
-            acc = psum.tile([SEQ, CHUNK], F32)
+            acc = psum.tile([SEQ, widths[c]], F32)
             nc.tensor.matmul_mx(
                 out=acc[:],
                 lhsT=x_codes[:].bitcast(FP8X4),
@@ -131,39 +133,41 @@ def tile_gqa_pa_s_kernel(tc, x, cos, sin, Wq, Wkv, out_0, out_1, out_2):
 
         products = {}
 
-        def multiply(c, first, heads):
-            product = work.tile([SEQ, 2, heads * HEAD], F32)
-            lanes = slice(first * HEAD, (first + heads) * HEAD)
+        def multiply(c):
+            heads = widths[c] // HEAD
+            product = work.tile([SEQ, 2, widths[c]], F32)
             nc.vector.tensor_tensor(
                 out=product[:].rearrange("p j (h d) -> p j h d", h=heads),
-                in0=banks[c][:, lanes].rearrange("p (h d) -> p h d", h=heads).unsqueeze(1).to_broadcast([SEQ, 2, heads, HEAD]),
+                in0=banks[c][:].rearrange("p (h d) -> p h d", h=heads).unsqueeze(1).to_broadcast([SEQ, 2, heads, HEAD]),
                 in1=factors[:].rearrange("p j i e -> p j (i e)").unsqueeze(2).to_broadcast([SEQ, 2, heads, HEAD]),
                 op=MULT,
             )
-            for h in range(first, first + heads):
-                products[c, h] = (product, h - first)
+            products[c] = product
 
-        def add_and_store(engine, c, result, first, heads):
-            product, place = products[c, first]
-            lanes = slice(place * HEAD, (place + heads) * HEAD)
-            engine.tensor_tensor(
-                out=result[:].rearrange("p (n e) -> p n e", e=2),
-                in0=product[:, 0, lanes].rearrange("p (n e) -> p n e", e=2),
-                in1=product[:, 1, lanes].rearrange("p (n e) -> p n e", e=2)[:, :, ::-1],
-                op=ADD,
-            )
+        def store(c, result, first, heads):
             nc.sync.dma_start(
                 out=chunks[c][1][first : first + heads].rearrange("h s d -> s h d"),
                 in_=result[:].rearrange("p (h d) -> p h d", h=heads),
             )
 
-        def combine_vector(c, first, heads):
+        def add_and_store(engine, c, result, first, heads):
+            lanes = slice(first * HEAD, (first + heads) * HEAD)
+            engine.tensor_tensor(
+                out=result[:].rearrange("p (n e) -> p n e", e=2),
+                in0=products[c][:, 0, lanes].rearrange("p (n e) -> p n e", e=2),
+                in1=products[c][:, 1, lanes].rearrange("p (n e) -> p n e", e=2)[:, :, ::-1],
+                op=ADD,
+            )
+            store(c, result, first, heads)
+
+        def combine_vector(c, first):
+            heads = widths[c] // HEAD - first
             result_v = work.tile([SEQ, heads * HEAD], F32)
             add_and_store(nc.vector, c, result_v, first, heads)
 
         def combine_gpsimd(c):
             result_g = overlay.tile(
-                [SEQ, GPSIMD_HEADS * HEAD], F32, name="result%d" % c, offset=(c + 2) * grouped_bytes, align_bytes=64
+                [SEQ, GPSIMD_HEADS * HEAD], F32, name="result%d" % c, offset=places[c + 2], align_bytes=64
             )
             add_and_store(nc.gpsimd, c, result_g, 0, GPSIMD_HEADS)
 
@@ -182,29 +186,25 @@ def tile_gqa_pa_s_kernel(tc, x, cos, sin, Wq, Wkv, out_0, out_1, out_2):
         regroup_scalar(2)
         project(1)
 
-        for c in range(n_chunks - 3):
-            multiply(c, 0, GROUP)
-            regroup_vector(c + 3)
-            regroup_scalar(c + 3)
-            combine_vector(c, GPSIMD_HEADS, GROUP - GPSIMD_HEADS)
+        values_at = Q_HEADS // GROUP
+        for c in range(values_at - 1):
+            multiply(c)
+            for ahead in range(c + 3, n_chunks if c + 3 == values_at + 1 else c + 4):
+                regroup_vector(ahead)
+                regroup_scalar(ahead)
+            combine_vector(c, GPSIMD_HEADS)
             project(c + 2)
             combine_gpsimd(c)
 
-        values_at = n_chunks - 2
         values = work.tile([SEQ, CHUNK], F32)
         nc.scalar.copy(out=values[:], in_=banks[values_at][:])
-        nc.sync.dma_start(
-            out=chunks[values_at][1].rearrange("h s d -> s h d"),
-            in_=values[:].rearrange("p (h d) -> p h d", h=GROUP),
-        )
+        store(values_at, values, 0, GROUP)
 
-        last = n_chunks - 1
-        multiply(values_at - 1, 0, GROUP)
-        project(last)
-        combine_vector(values_at - 1, 0, GROUP)
-
-        half = GROUP // 2
-        multiply(last, 0, half)
-        multiply(last, half, half)
-        combine_vector(last, 0, half)
-        combine_vector(last, half, half)
+        multiply(values_at - 1)
+        project(values_at + 1)
+        combine_vector(values_at - 1, 0)
+        project(values_at + 2)
+        multiply(values_at + 1)
+        multiply(values_at + 2)
+        combine_vector(values_at + 1, 0)
+        combine_vector(values_at + 2, 0)

@@ -21,7 +21,7 @@ Q_HEADS = 16
 KV_HEADS = 4
 GROUP = 4
 CHUNK = GROUP * HEAD
-RUN = 4
+RUN = 8
 
 VECTOR_COLS = (384, 256, 64, 64, 64, 32, 32)
 FIRST_LOAD = CHUNK // 2

@@ -24,7 +24,6 @@ CHUNK = GROUP * HEAD
 RUN = 8
 
 VECTOR_COLS = (384, 256, 64, 64, 64, 32, 32)
-FIRST_LOAD = CHUNK // 2
 GPSIMD_HEADS = 3
 
 FLOPS = 2 * SEQ * DIM * (Q_HEADS + 2 * KV_HEADS) * HEAD
@@ -35,13 +34,15 @@ def tile_gqa_pa_s_kernel(tc, x, cos, sin, Wq, Wkv, out_0, out_1, out_2):
 
     chunks = []
     for g in range(Q_HEADS // GROUP):
-        chunks.append((Wq[:, g * CHUNK : (g + 1) * CHUNK], out_0[0, g * GROUP : (g + 1) * GROUP], True))
-    chunks.append((Wkv[:, CHUNK : 2 * CHUNK], out_2[0], False))
+        chunks.append(out_0[0, g * GROUP : (g + 1) * GROUP])
+    chunks.append(out_2[0])
     half = GROUP // 2
     for g in range(2):
-        chunks.append((Wkv[:, g * half * HEAD : (g + 1) * half * HEAD], out_1[0, g * half : (g + 1) * half], True))
+        chunks.append(out_1[0, g * half : (g + 1) * half])
     n_chunks = len(chunks)
-    widths = [w_cols.shape[1] for w_cols, heads_out, rotated in chunks]
+    widths = [heads_out.shape[0] * HEAD for heads_out in chunks]
+    loads = [Wq[:, g * CHUNK : (g + 1) * CHUNK] for g in range(Q_HEADS // GROUP)]
+    loads += [Wkv[:, CHUNK : 2 * CHUNK], Wkv[:, 0:CHUNK]]
 
     with ExitStack() as ctx:
         const = ctx.enter_context(tc.tile_pool(name="const", bufs=1))
@@ -59,14 +60,13 @@ def tile_gqa_pa_s_kernel(tc, x, cos, sin, Wq, Wkv, out_0, out_1, out_2):
         sin_sb = const.tile([SEQ, PAIRS], BF16)
         nc.scalar.dma_start(out=sin_sb[:], in_=sin)
         raws = []
-        for c in range(n_chunks):
-            rows = chunks[c][0].rearrange("(p t) w -> p t w", t=PACK)
-            raw = weights.tile([P, PACK, widths[c]], BF16)
-            cut = FIRST_LOAD if c == 0 else 0
-            if cut:
-                nc.sync.dma_start(out=raw[:, :, 0:cut], in_=rows[:, :, 0:cut])
-            nc.sync.dma_start(out=raw[:, :, cut : widths[c]], in_=rows[:, :, cut : widths[c]])
+        for g in range(Q_HEADS // GROUP + 2):
+            raw = weights.tile([P, PACK, CHUNK], BF16)
+            nc.sync.dma_start(out=raw[:], in_=loads[g].rearrange("(p t) w -> p t w", t=PACK))
             raws.append(raw)
+        sources = [raws[c][:] for c in range(n_chunks - 2)]
+        for g in range(2):
+            sources.append(raws[n_chunks - 2][:, :, g * half * HEAD : (g + 1) * half * HEAD])
 
         warm = const.tile([P, 2], F32)
         nc.vector.memset(warm[:], 0.0)
@@ -94,15 +94,11 @@ def tile_gqa_pa_s_kernel(tc, x, cos, sin, Wq, Wkv, out_0, out_1, out_2):
         def regroup(copy, c, lo, hi):
             copy(
                 out=groupeds[c][:, lo:hi, :].rearrange("p (c i) t -> p c t i", i=RUN),
-                in_=raws[c][:, :, lo:hi].rearrange("p t (c i) -> p c t i", i=RUN),
+                in_=sources[c][:, :, lo:hi].rearrange("p t (c i) -> p c t i", i=RUN),
             )
 
         def regroup_vector(c):
-            if c == 0:
-                regroup(nc.vector.tensor_copy, c, 0, FIRST_LOAD)
-                regroup(nc.vector.tensor_copy, c, FIRST_LOAD, VECTOR_COLS[c])
-            else:
-                regroup(nc.vector.tensor_copy, c, 0, VECTOR_COLS[c])
+            regroup(nc.vector.tensor_copy, c, 0, VECTOR_COLS[c])
 
         def regroup_scalar(c):
             regroup(nc.scalar.copy, c, VECTOR_COLS[c], widths[c])
@@ -146,7 +142,7 @@ def tile_gqa_pa_s_kernel(tc, x, cos, sin, Wq, Wkv, out_0, out_1, out_2):
 
         def store(c, result, first, heads):
             nc.sync.dma_start(
-                out=chunks[c][1][first : first + heads].rearrange("h s d -> s h d"),
+                out=chunks[c][first : first + heads].rearrange("h s d -> s h d"),
                 in_=result[:].rearrange("p (h d) -> p h d", h=heads),
             )
 

@@ -23,8 +23,8 @@ GROUP = 4
 CHUNK = GROUP * HEAD
 RUN = 8
 
-VECTOR_COLS = (384, 256, 64, 64, 64, 32, 32)
-GPSIMD_HEADS = 3
+VECTOR_COLS = (384, 256, 128, 96, 64, 32, 0)
+GPSIMD_HEADS = (4, 3, 3, 3)
 
 FLOPS = 2 * SEQ * DIM * (Q_HEADS + 2 * KV_HEADS) * HEAD
 
@@ -98,7 +98,8 @@ def tile_gqa_pa_s_kernel(tc, x, cos, sin, Wq, Wkv, out_0, out_1, out_2):
             )
 
         def regroup_vector(c):
-            regroup(nc.vector.tensor_copy, c, 0, VECTOR_COLS[c])
+            if VECTOR_COLS[c]:
+                regroup(nc.vector.tensor_copy, c, 0, VECTOR_COLS[c])
 
         def regroup_scalar(c):
             regroup(nc.scalar.copy, c, VECTOR_COLS[c], widths[c])
@@ -163,9 +164,9 @@ def tile_gqa_pa_s_kernel(tc, x, cos, sin, Wq, Wkv, out_0, out_1, out_2):
 
         def combine_gpsimd(c):
             result_g = overlay.tile(
-                [SEQ, GPSIMD_HEADS * HEAD], F32, name="result%d" % c, offset=places[c + 2], align_bytes=64
+                [SEQ, GPSIMD_HEADS[c] * HEAD], F32, name="result%d" % c, offset=places[c + 2], align_bytes=64
             )
-            add_and_store(nc.gpsimd, c, result_g, 0, GPSIMD_HEADS)
+            add_and_store(nc.gpsimd, c, result_g, 0, GPSIMD_HEADS[c])
 
         regroup_vector(0)
         x_grouped = const.tile([P, SEQ * PACK], BF16, align_bytes=64)
@@ -183,22 +184,20 @@ def tile_gqa_pa_s_kernel(tc, x, cos, sin, Wq, Wkv, out_0, out_1, out_2):
         project(1)
 
         values_at = Q_HEADS // GROUP
-        for c in range(values_at - 1):
+        for c in range(values_at):
             multiply(c)
-            for ahead in range(c + 3, n_chunks if c + 3 == values_at + 1 else c + 4):
-                regroup_vector(ahead)
-                regroup_scalar(ahead)
-            combine_vector(c, GPSIMD_HEADS)
             project(c + 2)
+            regroup_vector(c + 3)
+            regroup_scalar(c + 3)
+            if c == values_at - 1:
+                values = work.tile([SEQ, CHUNK], F32)
+                nc.scalar.copy(out=values[:], in_=banks[values_at][:])
+            if GPSIMD_HEADS[c] < GROUP:
+                combine_vector(c, GPSIMD_HEADS[c])
+            if c == values_at - 1:
+                store(values_at, values, 0, GROUP)
             combine_gpsimd(c)
 
-        values = work.tile([SEQ, CHUNK], F32)
-        nc.scalar.copy(out=values[:], in_=banks[values_at][:])
-        store(values_at, values, 0, GROUP)
-
-        multiply(values_at - 1)
-        project(values_at + 1)
-        combine_vector(values_at - 1, 0)
         project(values_at + 2)
         multiply(values_at + 1)
         multiply(values_at + 2)

@@ -23,8 +23,9 @@ GROUP = 4
 CHUNK = GROUP * HEAD
 RUN = 8
 
-VECTOR_COLS = (384, 256, 128, 96, 64, 32, 0)
-GPSIMD_HEADS = (4, 3, 3, 3)
+VECTOR_COLS = (320, 320, 0, 128, 96, 0, 0)
+GPSIMD_COLS = (0, 0, 192, 0, 0, 0, 0)
+GPSIMD_HEADS = (2, 4, 2, 2)
 
 FLOPS = 2 * SEQ * DIM * (Q_HEADS + 2 * KV_HEADS) * HEAD
 
@@ -53,17 +54,18 @@ def tile_gqa_pa_s_kernel(tc, x, cos, sin, Wq, Wkv, out_0, out_1, out_2):
         psum = ctx.enter_context(tc.psum_pool(name="psum", bufs=n_chunks))
         ctx.enter_context(tc.manual_schedule())
 
-        x_sb = const.tile([SEQ, DIM], BF16)
-        nc.sync.dma_start(out=x_sb[:], in_=x[0])
-        cos_sb = const.tile([SEQ, PAIRS], BF16)
-        nc.scalar.dma_start(out=cos_sb[:], in_=cos)
-        sin_sb = const.tile([SEQ, PAIRS], BF16)
-        nc.scalar.dma_start(out=sin_sb[:], in_=sin)
         raws = []
         for g in range(Q_HEADS // GROUP + 2):
             raw = weights.tile([P, PACK, CHUNK], BF16)
             nc.sync.dma_start(out=raw[:], in_=loads[g].rearrange("(p t) w -> p t w", t=PACK))
             raws.append(raw)
+            if g == 0:
+                x_sb = const.tile([SEQ, DIM], BF16)
+                nc.sync.dma_start(out=x_sb[:], in_=x[0])
+                cos_sb = const.tile([SEQ, PAIRS], BF16)
+                nc.sync.dma_start(out=cos_sb[:], in_=cos)
+                sin_sb = const.tile([SEQ, PAIRS], BF16)
+                nc.sync.dma_start(out=sin_sb[:], in_=sin)
         sources = [raws[c][:] for c in range(n_chunks - 2)]
         for g in range(2):
             sources.append(raws[n_chunks - 2][:, :, g * half * HEAD : (g + 1) * half * HEAD])
@@ -78,11 +80,6 @@ def tile_gqa_pa_s_kernel(tc, x, cos, sin, Wq, Wkv, out_0, out_1, out_2):
         x_t = psum_x.tile([P, 2, SEQ], F32)
         for u in range(2):
             nc.tensor.transpose(x_t[:, u, :], x_words[:, u, :], ident[:])
-
-        factors = const.tile([SEQ, 2, PAIRS, 2], BF16)
-        nc.scalar.copy(out=factors[:, 0, :, :], in_=cos_sb[:].unsqueeze(2).to_broadcast([SEQ, PAIRS, 2]))
-        nc.scalar.copy(out=factors[:, 1, :, 0], in_=sin_sb[:])
-        nc.scalar.mul(out=factors[:, 1, :, 1], in_=sin_sb[:], mul=-1.0)
 
         places = [sum(widths[:c]) * PACK * 2 for c in range(n_chunks)]
         groupeds = []
@@ -101,14 +98,28 @@ def tile_gqa_pa_s_kernel(tc, x, cos, sin, Wq, Wkv, out_0, out_1, out_2):
             if VECTOR_COLS[c]:
                 regroup(nc.vector.tensor_copy, c, 0, VECTOR_COLS[c])
 
+        def regroup_gpsimd(c):
+            lo = VECTOR_COLS[c]
+            hi = lo + GPSIMD_COLS[c]
+            nc.gpsimd.tensor_scalar(
+                out=groupeds[c][:, lo:hi, :],
+                in0=sources[c][:, :, lo:hi].rearrange("p t c -> p c t"),
+                scalar1=1.0,
+                scalar2=0.0,
+                op0=MULT,
+                op1=ADD,
+            )
+
         def regroup_scalar(c):
-            regroup(nc.scalar.copy, c, VECTOR_COLS[c], widths[c])
+            regroup(nc.scalar.copy, c, VECTOR_COLS[c] + GPSIMD_COLS[c], widths[c])
 
         x_codes = const.tile([P, SEQ], U32, align_bytes=64)
         x_scales = const.tile([P, SEQ], U8, align_bytes=64)
         banks = {}
 
-        def project(c):
+        quantised = {}
+
+        def quantise(c):
             codes = weights.tile([P, widths[c]], U32, align_bytes=64)
             scales = weights.tile([P, widths[c]], U8, align_bytes=64)
             nc.vector.quantize_mx(
@@ -116,6 +127,10 @@ def tile_gqa_pa_s_kernel(tc, x, cos, sin, Wq, Wkv, out_0, out_1, out_2):
                 scales=scales[:],
                 in_=groupeds[c][:].rearrange("p w t -> p (w t)"),
             )
+            quantised[c] = (codes, scales)
+
+        def project(c):
+            codes, scales = quantised[c]
             acc = psum.tile([SEQ, widths[c]], F32)
             nc.tensor.matmul_mx(
                 out=acc[:],
@@ -162,44 +177,71 @@ def tile_gqa_pa_s_kernel(tc, x, cos, sin, Wq, Wkv, out_0, out_1, out_2):
             result_v = work.tile([SEQ, heads * HEAD], F32)
             add_and_store(nc.vector, c, result_v, first, heads)
 
-        def combine_gpsimd(c):
-            result_g = overlay.tile(
-                [SEQ, GPSIMD_HEADS[c] * HEAD], F32, name="result%d" % c, offset=places[c + 2], align_bytes=64
-            )
-            add_and_store(nc.gpsimd, c, result_g, 0, GPSIMD_HEADS[c])
+        def combine_gpsimd(c, over=None):
+            heads = GPSIMD_HEADS[c]
+            if over is None:
+                result_g = work.tile([SEQ, heads * HEAD], F32)
+            else:
+                result_g = overlay.tile(
+                    [SEQ, heads * HEAD], F32, name="result%d" % c, offset=places[over], align_bytes=64
+                )
+            add_and_store(nc.gpsimd, c, result_g, 0, heads)
 
         regroup_vector(0)
+        regroup_scalar(0)
         x_grouped = const.tile([P, SEQ * PACK], BF16, align_bytes=64)
         nc.scalar.copy(
             out=x_grouped[:].bitcast(F32).rearrange("p (s u) -> p s u", u=2),
             in_=x_t[:].rearrange("p u s -> p s u"),
         )
-        regroup_scalar(0)
+        factors = const.tile([SEQ, 2, PAIRS, 2], BF16)
+        nc.scalar.copy(out=factors[:, 0, :, :], in_=cos_sb[:].unsqueeze(2).to_broadcast([SEQ, PAIRS, 2]))
+        nc.scalar.copy(out=factors[:, 1, :, 0], in_=sin_sb[:])
+        nc.scalar.mul(out=factors[:, 1, :, 1], in_=sin_sb[:], mul=-1.0)
+
+        quantise(0)
         nc.vector.quantize_mx(out=x_codes[:].bitcast(FP8X4), scales=x_scales[:], in_=x_grouped[:])
         project(0)
         regroup_vector(1)
         regroup_scalar(1)
-        regroup_vector(2)
-        regroup_scalar(2)
+        quantise(1)
         project(1)
+        regroup_gpsimd(2)
+        regroup_scalar(2)
 
-        values_at = Q_HEADS // GROUP
-        for c in range(values_at):
-            multiply(c)
-            project(c + 2)
-            regroup_vector(c + 3)
-            regroup_scalar(c + 3)
-            if c == values_at - 1:
-                values = work.tile([SEQ, CHUNK], F32)
-                nc.scalar.copy(out=values[:], in_=banks[values_at][:])
-            if GPSIMD_HEADS[c] < GROUP:
-                combine_vector(c, GPSIMD_HEADS[c])
-            if c == values_at - 1:
-                store(values_at, values, 0, GROUP)
-            combine_gpsimd(c)
+        multiply(0)
+        combine_gpsimd(0)
+        multiply(1)
+        quantise(2)
+        project(2)
+        regroup_vector(3)
+        regroup_scalar(3)
+        combine_vector(0, GPSIMD_HEADS[0])
+        quantise(3)
+        project(3)
+        combine_gpsimd(1, over=3)
+        regroup_vector(4)
+        for c in range(4, n_chunks):
+            regroup_scalar(c)
 
-        project(values_at + 2)
-        multiply(values_at + 1)
-        multiply(values_at + 2)
-        combine_vector(values_at + 1, 0)
-        combine_vector(values_at + 2, 0)
+        multiply(2)
+        combine_gpsimd(2)
+        multiply(3)
+        quantise(4)
+        project(4)
+        quantise(5)
+        project(5)
+        combine_vector(3, GPSIMD_HEADS[3])
+        combine_vector(2, GPSIMD_HEADS[2])
+
+        values = work.tile([SEQ, CHUNK], F32)
+        nc.scalar.copy(out=values[:], in_=banks[4][:])
+        store(4, values, 0, GROUP)
+
+        quantise(6)
+        project(6)
+        combine_gpsimd(3, over=6)
+        multiply(5)
+        multiply(6)
+        combine_vector(5, 0)
+        combine_vector(6, 0)

@@ -23,8 +23,8 @@ GROUP = 4
 CHUNK = GROUP * HEAD
 RUN = 8
 
-VECTOR_COLS = (320, 320, 0, 128, 96, 0, 0)
-GPSIMD_COLS = (0, 0, 192, 0, 0, 0, 0)
+VECTOR_COLS = (352, 320, 0, 128, 0, 0, 0, 0)
+GPSIMD_COLS = (0, 0, 256, 0, 0, 0, 0, 0)
 GPSIMD_HEADS = (2, 4, 2, 2)
 
 FLOPS = 2 * SEQ * DIM * (Q_HEADS + 2 * KV_HEADS) * HEAD
@@ -37,9 +37,10 @@ def tile_gqa_pa_s_kernel(tc, x, cos, sin, Wq, Wkv, out_0, out_1, out_2):
     for g in range(Q_HEADS // GROUP):
         chunks.append(out_0[0, g * GROUP : (g + 1) * GROUP])
     chunks.append(out_2[0])
-    half = GROUP // 2
-    for g in range(2):
-        chunks.append(out_1[0, g * half : (g + 1) * half])
+    first_key_chunk = len(chunks)
+    key_heads = ((0, 2), (2, 3), (3, 4))
+    for first, last in key_heads:
+        chunks.append(out_1[0, first:last])
     n_chunks = len(chunks)
     widths = [heads_out.shape[0] * HEAD for heads_out in chunks]
     loads = [Wq[:, g * CHUNK : (g + 1) * CHUNK] for g in range(Q_HEADS // GROUP)]
@@ -51,7 +52,7 @@ def tile_gqa_pa_s_kernel(tc, x, cos, sin, Wq, Wkv, out_0, out_1, out_2):
         work = ctx.enter_context(tc.tile_pool(name="work", bufs=n_chunks))
         overlay = ctx.enter_context(tc.tile_pool(name="overlay", bufs=1))
         psum_x = ctx.enter_context(tc.psum_pool(name="psum_x", bufs=1))
-        psum = ctx.enter_context(tc.psum_pool(name="psum", bufs=n_chunks))
+        psum = ctx.enter_context(tc.psum_pool(name="psum", bufs=7))
         ctx.enter_context(tc.manual_schedule())
 
         raws = []
@@ -66,9 +67,9 @@ def tile_gqa_pa_s_kernel(tc, x, cos, sin, Wq, Wkv, out_0, out_1, out_2):
                 nc.sync.dma_start(out=cos_sb[:], in_=cos)
                 sin_sb = const.tile([SEQ, PAIRS], BF16)
                 nc.sync.dma_start(out=sin_sb[:], in_=sin)
-        sources = [raws[c][:] for c in range(n_chunks - 2)]
-        for g in range(2):
-            sources.append(raws[n_chunks - 2][:, :, g * half * HEAD : (g + 1) * half * HEAD])
+        sources = [raws[c][:] for c in range(first_key_chunk)]
+        for first, last in key_heads:
+            sources.append(raws[first_key_chunk][:, :, first * HEAD : last * HEAD])
 
         warm = const.tile([P, 2], F32)
         nc.vector.memset(warm[:], 0.0)
@@ -220,7 +221,6 @@ def tile_gqa_pa_s_kernel(tc, x, cos, sin, Wq, Wkv, out_0, out_1, out_2):
         quantise(3)
         project(3)
         combine_gpsimd(1, over=3)
-        regroup_vector(4)
         for c in range(4, n_chunks):
             regroup_scalar(c)
 
@@ -240,8 +240,12 @@ def tile_gqa_pa_s_kernel(tc, x, cos, sin, Wq, Wkv, out_0, out_1, out_2):
 
         quantise(6)
         project(6)
-        combine_gpsimd(3, over=6)
+        quantise(7)
+        project(7)
+        combine_gpsimd(3, over=7)
         multiply(5)
         multiply(6)
         combine_vector(5, 0)
+        multiply(7)
         combine_vector(6, 0)
+        combine_vector(7, 0)

@@ -10,6 +10,7 @@ U8 = mybir.dt.uint8
 FP8X4 = mybir.dt.float8_e4m3fn_x4
 MULT = mybir.AluOpType.mult
 ADD = mybir.AluOpType.add
+SUB = mybir.AluOpType.subtract
 
 P = 128
 PACK = 4
@@ -22,10 +23,12 @@ KV_HEADS = 4
 GROUP = 4
 CHUNK = GROUP * HEAD
 RUN = 8
+VALUES = Q_HEADS // GROUP
+KEYS = VALUES + 1
 
-VECTOR_COLS = (352, 320, 0, 128, 0, 0, 0, 0)
-GPSIMD_COLS = (0, 0, 256, 0, 0, 0, 0, 0)
-GPSIMD_HEADS = (2, 4, 2, 2)
+VECTOR_COLS = (320, 320, 0, 352, 0, 0, 0)
+GPSIMD_COLS = (0, 0, 128, 0, 0, 0, 0)
+GPSIMD_HEADS = (2, 3, 2, 2)
 
 FLOPS = 2 * SEQ * DIM * (Q_HEADS + 2 * KV_HEADS) * HEAD
 
@@ -33,17 +36,13 @@ FLOPS = 2 * SEQ * DIM * (Q_HEADS + 2 * KV_HEADS) * HEAD
 def tile_gqa_pa_s_kernel(tc, x, cos, sin, Wq, Wkv, out_0, out_1, out_2):
     nc = tc.nc
 
-    chunks = []
-    for g in range(Q_HEADS // GROUP):
-        chunks.append(out_0[0, g * GROUP : (g + 1) * GROUP])
+    half = GROUP // 2
+    chunks = [out_0[0, g * GROUP : (g + 1) * GROUP] for g in range(VALUES)]
     chunks.append(out_2[0])
-    first_key_chunk = len(chunks)
-    key_heads = ((0, 2), (2, 3), (3, 4))
-    for first, last in key_heads:
-        chunks.append(out_1[0, first:last])
+    chunks += [out_1[0, g * half : (g + 1) * half] for g in range(2)]
     n_chunks = len(chunks)
     widths = [heads_out.shape[0] * HEAD for heads_out in chunks]
-    loads = [Wq[:, g * CHUNK : (g + 1) * CHUNK] for g in range(Q_HEADS // GROUP)]
+    loads = [Wq[:, g * CHUNK : (g + 1) * CHUNK] for g in range(VALUES)]
     loads += [Wkv[:, CHUNK : 2 * CHUNK], Wkv[:, 0:CHUNK]]
 
     with ExitStack() as ctx:
@@ -52,11 +51,12 @@ def tile_gqa_pa_s_kernel(tc, x, cos, sin, Wq, Wkv, out_0, out_1, out_2):
         work = ctx.enter_context(tc.tile_pool(name="work", bufs=n_chunks))
         overlay = ctx.enter_context(tc.tile_pool(name="overlay", bufs=1))
         psum_x = ctx.enter_context(tc.psum_pool(name="psum_x", bufs=1))
-        psum = ctx.enter_context(tc.psum_pool(name="psum", bufs=7))
+        psum = ctx.enter_context(tc.psum_pool(name="psum", bufs=4))
+        psum_sums = ctx.enter_context(tc.psum_pool(name="psum_sums", bufs=3))
         ctx.enter_context(tc.manual_schedule())
 
         raws = []
-        for g in range(Q_HEADS // GROUP + 2):
+        for g in range(len(loads)):
             raw = weights.tile([P, PACK, CHUNK], BF16)
             nc.sync.dma_start(out=raw[:], in_=loads[g].rearrange("(p t) w -> p t w", t=PACK))
             raws.append(raw)
@@ -67,9 +67,9 @@ def tile_gqa_pa_s_kernel(tc, x, cos, sin, Wq, Wkv, out_0, out_1, out_2):
                 nc.sync.dma_start(out=cos_sb[:], in_=cos)
                 sin_sb = const.tile([SEQ, PAIRS], BF16)
                 nc.sync.dma_start(out=sin_sb[:], in_=sin)
-        sources = [raws[c][:] for c in range(first_key_chunk)]
-        for first, last in key_heads:
-            sources.append(raws[first_key_chunk][:, :, first * HEAD : last * HEAD])
+        sources = [raws[c][:] for c in range(KEYS)]
+        for g in range(2):
+            sources.append(raws[KEYS][:, :, g * half * HEAD : (g + 1) * half * HEAD])
 
         warm = const.tile([P, 2], F32)
         nc.vector.memset(warm[:], 0.0)
@@ -89,35 +89,27 @@ def tile_gqa_pa_s_kernel(tc, x, cos, sin, Wq, Wkv, out_0, out_1, out_2):
                 overlay.tile([P, widths[c], PACK], BF16, name="grouped%d" % c, offset=places[c], align_bytes=64)
             )
 
-        def regroup(copy, c, lo, hi):
-            copy(
-                out=groupeds[c][:, lo:hi, :].rearrange("p (c i) t -> p c t i", i=RUN),
-                in_=sources[c][:, :, lo:hi].rearrange("p t (c i) -> p c t i", i=RUN),
-            )
+        def views(c, lo, hi):
+            if c == VALUES:
+                out = groupeds[c][:, lo:hi, :].rearrange("p (c i) t -> p c t i", i=RUN)
+                return out, sources[c][:, :, lo:hi].rearrange("p t (c i) -> p c t i", i=RUN)
+            out = groupeds[c][:].rearrange("p (e n) t -> p e n t", e=2)[:, :, lo // 2 : hi // 2, :]
+            return out, sources[c][:, :, lo:hi].rearrange("p t (n e) -> p e n t", e=2)
 
         def regroup_vector(c):
-            if VECTOR_COLS[c]:
-                regroup(nc.vector.tensor_copy, c, 0, VECTOR_COLS[c])
+            out, in_ = views(c, 0, VECTOR_COLS[c])
+            nc.vector.tensor_copy(out=out, in_=in_)
 
         def regroup_gpsimd(c):
-            lo = VECTOR_COLS[c]
-            hi = lo + GPSIMD_COLS[c]
-            nc.gpsimd.tensor_scalar(
-                out=groupeds[c][:, lo:hi, :],
-                in0=sources[c][:, :, lo:hi].rearrange("p t c -> p c t"),
-                scalar1=1.0,
-                scalar2=0.0,
-                op0=MULT,
-                op1=ADD,
-            )
+            out, in_ = views(c, VECTOR_COLS[c], VECTOR_COLS[c] + GPSIMD_COLS[c])
+            nc.gpsimd.tensor_scalar(out=out, in0=in_, scalar1=1.0, scalar2=0.0, op0=MULT, op1=ADD)
 
         def regroup_scalar(c):
-            regroup(nc.scalar.copy, c, VECTOR_COLS[c] + GPSIMD_COLS[c], widths[c])
+            out, in_ = views(c, VECTOR_COLS[c] + GPSIMD_COLS[c], widths[c])
+            nc.scalar.copy(out=out, in_=in_)
 
         x_codes = const.tile([P, SEQ], U32, align_bytes=64)
         x_scales = const.tile([P, SEQ], U8, align_bytes=64)
-        banks = {}
-
         quantised = {}
 
         def quantise(c):
@@ -130,31 +122,51 @@ def tile_gqa_pa_s_kernel(tc, x, cos, sin, Wq, Wkv, out_0, out_1, out_2):
             )
             quantised[c] = (codes, scales)
 
-        def project(c):
+        def pass_mx(c, out, lo, hi, start, stop):
             codes, scales = quantised[c]
-            acc = psum.tile([SEQ, widths[c]], F32)
             nc.tensor.matmul_mx(
-                out=acc[:],
+                out=out,
                 lhsT=x_codes[:].bitcast(FP8X4),
                 lhsT_scale=x_scales[:],
-                rhs=codes[:].bitcast(FP8X4),
-                rhs_scale=scales[:],
-                start=True,
-                stop=True,
+                rhs=codes[:, lo:hi].bitcast(FP8X4),
+                rhs_scale=scales[:, lo:hi],
+                start=start,
+                stop=stop,
             )
-            banks[c] = acc
 
+        banks = {}
+
+        def project(c):
+            width = widths[c]
+            acc = psum.tile([SEQ, CHUNK], F32)
+            pass_mx(c, acc[:, 0:width], 0, width, True, True)
+            banks[c] = [(acc[:, 0:width], 0)]
+            if c == VALUES:
+                return
+            if width == CHUNK:
+                sums_bank = psum_sums.tile([SEQ, CHUNK], F32)
+                sums = sums_bank[:, 0 : width // 2]
+                banks[c].append((sums, 2))
+            else:
+                sums = acc[:, width : width + width // 2]
+                banks[c] = [(acc[:, 0 : width + width // 2], 0)]
+            for e in range(2):
+                pass_mx(c, sums, e * (width // 2), (e + 1) * (width // 2), e == 0, e == 1)
+
+        factors = const.tile([SEQ, 3, PAIRS], F32)
         products = {}
 
         def multiply(c):
             heads = widths[c] // HEAD
-            product = work.tile([SEQ, 2, widths[c]], F32)
-            nc.vector.tensor_tensor(
-                out=product[:].rearrange("p j (h d) -> p j h d", h=heads),
-                in0=banks[c][:].rearrange("p (h d) -> p h d", h=heads).unsqueeze(1).to_broadcast([SEQ, 2, heads, HEAD]),
-                in1=factors[:].rearrange("p j i e -> p j (i e)").unsqueeze(2).to_broadcast([SEQ, 2, heads, HEAD]),
-                op=MULT,
-            )
+            product = work.tile([SEQ, 3, heads * PAIRS], F32)
+            for bank, row in banks[c]:
+                rows = bank.shape[1] // (heads * PAIRS)
+                nc.vector.tensor_tensor(
+                    out=product[:, row : row + rows, :].rearrange("p j (h i) -> p j h i", h=heads),
+                    in0=bank.rearrange("p (j h i) -> p j h i", j=rows, h=heads),
+                    in1=factors[:, row : row + rows, :].unsqueeze(2).to_broadcast([SEQ, rows, heads, PAIRS]),
+                    op=MULT,
+                )
             products[c] = product
 
         def store(c, result, first, heads):
@@ -164,11 +176,11 @@ def tile_gqa_pa_s_kernel(tc, x, cos, sin, Wq, Wkv, out_0, out_1, out_2):
             )
 
         def add_and_store(engine, c, result, first, heads):
-            lanes = slice(first * HEAD, (first + heads) * HEAD)
+            pairs = slice(first * PAIRS, (first + heads) * PAIRS)
             engine.tensor_tensor(
                 out=result[:].rearrange("p (n e) -> p n e", e=2),
-                in0=products[c][:, 0, lanes].rearrange("p (n e) -> p n e", e=2),
-                in1=products[c][:, 1, lanes].rearrange("p (n e) -> p n e", e=2)[:, :, ::-1],
+                in0=products[c][:, 2, pairs].unsqueeze(2).to_broadcast([SEQ, heads * PAIRS, 2]),
+                in1=products[c][:, 0:2, pairs].rearrange("p e n -> p n e")[:, :, ::-1],
                 op=ADD,
             )
             store(c, result, first, heads)
@@ -178,14 +190,9 @@ def tile_gqa_pa_s_kernel(tc, x, cos, sin, Wq, Wkv, out_0, out_1, out_2):
             result_v = work.tile([SEQ, heads * HEAD], F32)
             add_and_store(nc.vector, c, result_v, first, heads)
 
-        def combine_gpsimd(c, over=None):
+        def combine_gpsimd(c, over):
             heads = GPSIMD_HEADS[c]
-            if over is None:
-                result_g = work.tile([SEQ, heads * HEAD], F32)
-            else:
-                result_g = overlay.tile(
-                    [SEQ, heads * HEAD], F32, name="result%d" % c, offset=places[over], align_bytes=64
-                )
+            result_g = overlay.tile([SEQ, heads * HEAD], F32, name="result%d" % c, offset=places[over], align_bytes=64)
             add_and_store(nc.gpsimd, c, result_g, 0, heads)
 
         regroup_vector(0)
@@ -195,57 +202,43 @@ def tile_gqa_pa_s_kernel(tc, x, cos, sin, Wq, Wkv, out_0, out_1, out_2):
             out=x_grouped[:].bitcast(F32).rearrange("p (s u) -> p s u", u=2),
             in_=x_t[:].rearrange("p u s -> p s u"),
         )
-        factors = const.tile([SEQ, 2, PAIRS, 2], BF16)
-        nc.scalar.copy(out=factors[:, 0, :, :], in_=cos_sb[:].unsqueeze(2).to_broadcast([SEQ, PAIRS, 2]))
-        nc.scalar.copy(out=factors[:, 1, :, 0], in_=sin_sb[:])
-        nc.scalar.mul(out=factors[:, 1, :, 1], in_=sin_sb[:], mul=-1.0)
-
+        nc.scalar.copy(out=factors[:, 2, :], in_=cos_sb[:])
         quantise(0)
         nc.vector.quantize_mx(out=x_codes[:].bitcast(FP8X4), scales=x_scales[:], in_=x_grouped[:])
         project(0)
         regroup_vector(1)
         regroup_scalar(1)
+        nc.vector.tensor_tensor(out=factors[:, 0, :], in0=sin_sb[:], in1=cos_sb[:], op=SUB)
+        nc.vector.scalar_tensor_tensor(
+            out=factors[:, 1, :], in0=cos_sb[:], scalar=-1.0, in1=sin_sb[:], op0=MULT, op1=SUB
+        )
         quantise(1)
         project(1)
         regroup_gpsimd(2)
         regroup_scalar(2)
 
-        multiply(0)
-        combine_gpsimd(0)
-        multiply(1)
-        quantise(2)
-        project(2)
-        regroup_vector(3)
-        regroup_scalar(3)
-        combine_vector(0, GPSIMD_HEADS[0])
-        quantise(3)
-        project(3)
-        combine_gpsimd(1, over=3)
-        for c in range(4, n_chunks):
-            regroup_scalar(c)
-
-        multiply(2)
-        combine_gpsimd(2)
-        multiply(3)
-        quantise(4)
-        project(4)
-        quantise(5)
-        project(5)
-        combine_vector(3, GPSIMD_HEADS[3])
-        combine_vector(2, GPSIMD_HEADS[2])
+        for c in range(VALUES):
+            multiply(c)
+            if c == 0:
+                regroup_vector(3)
+                for later in range(3, n_chunks):
+                    regroup_scalar(later)
+            quantise(c + 2)
+            project(c + 2)
+            if c > 0:
+                combine_vector(c - 1, GPSIMD_HEADS[c - 1])
+            if c < VALUES - 1:
+                combine_gpsimd(c, c + 2)
 
         values = work.tile([SEQ, CHUNK], F32)
-        nc.scalar.copy(out=values[:], in_=banks[4][:])
-        store(4, values, 0, GROUP)
+        nc.scalar.copy(out=values[:], in_=banks[VALUES][0][0])
+        store(VALUES, values, 0, GROUP)
 
-        quantise(6)
-        project(6)
-        quantise(7)
-        project(7)
-        combine_gpsimd(3, over=7)
-        multiply(5)
-        multiply(6)
-        combine_vector(5, 0)
-        multiply(7)
-        combine_vector(6, 0)
-        combine_vector(7, 0)
+        quantise(KEYS + 1)
+        project(KEYS + 1)
+        combine_vector(VALUES - 1, GPSIMD_HEADS[VALUES - 1])
+        combine_gpsimd(VALUES - 1, KEYS + 1)
+        multiply(KEYS)
+        multiply(KEYS + 1)
+        combine_vector(KEYS, 0)
+        combine_vector(KEYS + 1, 0)

@@ -91,17 +91,21 @@ def tile_gqa_pa_s_kernel(tc, x, cos, sin, Wq, Wkv, out_0, out_1, out_2):
 
         def views(c, lo, hi):
             if c == VALUES:
-                out = groupeds[c][:, lo:hi, :].rearrange("p (c i) t -> p c t i", i=RUN)
-                return out, sources[c][:, :, lo:hi].rearrange("p t (c i) -> p c t i", i=RUN)
-            out = groupeds[c][:].rearrange("p (e n) t -> p e n t", e=2)[:, :, lo // 2 : hi // 2, :]
-            return out, sources[c][:, :, lo:hi].rearrange("p t (n e) -> p e n t", e=2)
+                out = groupeds[c][:, lo:hi, :].rearrange("p (b i) t -> p b t i", i=RUN)
+                return out, sources[c][:, :, lo:hi].rearrange("p t (b i) -> p b t i", i=RUN)
+            out = groupeds[c][:].rearrange("p (e b n) t -> p b t n e", e=2, n=RUN // 2)
+            in_ = sources[c][:].rearrange("p t (b n e) -> p b t n e", e=2, n=RUN // 2)
+            blocks = slice(lo // RUN, hi // RUN)
+            return out[:, blocks], in_[:, blocks]
 
         def regroup_vector(c):
             out, in_ = views(c, 0, VECTOR_COLS[c])
             nc.vector.tensor_copy(out=out, in_=in_)
 
         def regroup_gpsimd(c):
-            out, in_ = views(c, VECTOR_COLS[c], VECTOR_COLS[c] + GPSIMD_COLS[c])
+            pairs = slice(VECTOR_COLS[c] // 2, (VECTOR_COLS[c] + GPSIMD_COLS[c]) // 2)
+            out = groupeds[c][:].rearrange("p (e n) t -> p e n t", e=2)[:, :, pairs]
+            in_ = sources[c][:].rearrange("p t (n e) -> p e n t", e=2)[:, :, pairs]
             nc.gpsimd.tensor_scalar(out=out, in0=in_, scalar1=1.0, scalar2=0.0, op0=MULT, op1=ADD)
 
         def regroup_scalar(c):

@@ -26,9 +26,9 @@ RUN = 8
 VALUES = Q_HEADS // GROUP
 KEYS = VALUES + 1
 
-VECTOR_COLS = (320, 320, 0, 352, 0, 0, 0)
-GPSIMD_COLS = (0, 0, 128, 0, 0, 0, 0)
-GPSIMD_HEADS = (2, 3, 2, 2)
+VECTOR_COLS = (320, 320, 0, 320, 0, 0, 0)
+GPSIMD_COLS = (0, 0, 160, 0, 0, 0, 0)
+GPSIMD_HEADS = (4, 3, 3, 2)
 
 FLOPS = 2 * SEQ * DIM * (Q_HEADS + 2 * KV_HEADS) * HEAD
 
@@ -147,13 +147,9 @@ def tile_gqa_pa_s_kernel(tc, x, cos, sin, Wq, Wkv, out_0, out_1, out_2):
             banks[c] = [(acc[:, 0:width], 0)]
             if c == VALUES:
                 return
-            if width == CHUNK:
-                sums_bank = psum_sums.tile([SEQ, CHUNK], F32)
-                sums = sums_bank[:, 0 : width // 2]
-                banks[c].append((sums, 2))
-            else:
-                sums = acc[:, width : width + width // 2]
-                banks[c] = [(acc[:, 0 : width + width // 2], 0)]
+            sums_bank = psum_sums.tile([SEQ, CHUNK], F32)
+            sums = sums_bank[:, 0 : width // 2]
+            banks[c].append((sums, 2))
             for e in range(2):
                 pass_mx(c, sums, e * (width // 2), (e + 1) * (width // 2), e == 0, e == 1)
 
@@ -194,9 +190,14 @@ def tile_gqa_pa_s_kernel(tc, x, cos, sin, Wq, Wkv, out_0, out_1, out_2):
             result_v = work.tile([SEQ, heads * HEAD], F32)
             add_and_store(nc.vector, c, result_v, first, heads)
 
-        def combine_gpsimd(c, over):
+        def combine_gpsimd(c, over=None):
             heads = GPSIMD_HEADS[c]
-            result_g = overlay.tile([SEQ, heads * HEAD], F32, name="result%d" % c, offset=places[over], align_bytes=64)
+            if over is None:
+                result_g = work.tile([SEQ, heads * HEAD], F32)
+            else:
+                result_g = overlay.tile(
+                    [SEQ, heads * HEAD], F32, name="result%d" % c, offset=places[over], align_bytes=64
+                )
             add_and_store(nc.gpsimd, c, result_g, 0, heads)
 
         regroup_vector(0)
@@ -207,42 +208,50 @@ def tile_gqa_pa_s_kernel(tc, x, cos, sin, Wq, Wkv, out_0, out_1, out_2):
             in_=x_t[:].rearrange("p u s -> p s u"),
         )
         nc.scalar.copy(out=factors[:, 2, :], in_=cos_sb[:])
+        nc.vector.tensor_tensor(out=factors[:, 0, :], in0=sin_sb[:], in1=cos_sb[:], op=SUB)
+        nc.vector.scalar_tensor_tensor(
+            out=factors[:, 1, :], in0=cos_sb[:], scalar=-1.0, in1=sin_sb[:], op0=MULT, op1=SUB
+        )
         quantise(0)
         nc.vector.quantize_mx(out=x_codes[:].bitcast(FP8X4), scales=x_scales[:], in_=x_grouped[:])
         project(0)
         regroup_vector(1)
         regroup_scalar(1)
-        nc.vector.tensor_tensor(out=factors[:, 0, :], in0=sin_sb[:], in1=cos_sb[:], op=SUB)
-        nc.vector.scalar_tensor_tensor(
-            out=factors[:, 1, :], in0=cos_sb[:], scalar=-1.0, in1=sin_sb[:], op0=MULT, op1=SUB
-        )
         quantise(1)
         project(1)
         regroup_gpsimd(2)
         regroup_scalar(2)
 
-        for c in range(VALUES):
-            multiply(c)
-            if c == 0:
-                regroup_vector(3)
-                for later in range(3, n_chunks):
-                    regroup_scalar(later)
-            quantise(c + 2)
-            project(c + 2)
-            if c > 0:
-                combine_vector(c - 1, GPSIMD_HEADS[c - 1])
-            if c < VALUES - 1:
-                combine_gpsimd(c, c + 2)
+        multiply(0)
+        regroup_vector(3)
+        for later in range(3, n_chunks):
+            regroup_scalar(later)
+        quantise(2)
+        project(2)
+        combine_gpsimd(0, over=2)
+        quantise(3)
+        project(3)
+        multiply(1)
+        combine_gpsimd(1)
+        multiply(2)
+        quantise(4)
+        project(4)
+        multiply(3)
+        combine_vector(2, GPSIMD_HEADS[2])
+        combine_gpsimd(2)
+        quantise(5)
+        project(5)
+        combine_vector(3, GPSIMD_HEADS[3])
 
         values = work.tile([SEQ, CHUNK], F32)
         nc.scalar.copy(out=values[:], in_=banks[VALUES][0][0])
         store(VALUES, values, 0, GROUP)
 
-        quantise(KEYS + 1)
-        project(KEYS + 1)
-        combine_vector(VALUES - 1, GPSIMD_HEADS[VALUES - 1])
-        combine_gpsimd(VALUES - 1, KEYS + 1)
-        multiply(KEYS)
-        multiply(KEYS + 1)
-        combine_vector(KEYS, 0)
-        combine_vector(KEYS + 1, 0)
+        quantise(6)
+        project(6)
+        combine_vector(1, GPSIMD_HEADS[1])
+        combine_gpsimd(3, over=6)
+        multiply(5)
+        multiply(6)
+        combine_vector(5, 0)
+        combine_vector(6, 0)

@@ -139,35 +139,41 @@ def tile_gqa_pa_s_kernel(tc, x, cos, sin, Wq, Wkv, out_0, out_1, out_2):
             )
 
         banks = {}
+        sums = {}
 
         def project(c):
             width = widths[c]
             acc = psum.tile([SEQ, CHUNK], F32)
             pass_mx(c, acc[:, 0:width], 0, width, True, True)
-            banks[c] = [(acc[:, 0:width], 0)]
+            banks[c] = acc[:, 0:width]
             if c == VALUES:
                 return
             sums_bank = psum_sums.tile([SEQ, CHUNK], F32)
-            sums = sums_bank[:, 0 : width // 2]
-            banks[c].append((sums, 2))
+            sums[c] = sums_bank[:, 0 : width // 2]
             for e in range(2):
-                pass_mx(c, sums, e * (width // 2), (e + 1) * (width // 2), e == 0, e == 1)
+                pass_mx(c, sums[c], e * (width // 2), (e + 1) * (width // 2), e == 0, e == 1)
 
-        factors = const.tile([SEQ, 3, PAIRS], F32)
+        crossed = const.tile([SEQ, PAIRS, 2], F32)
+        cos_f32 = const.tile([SEQ, PAIRS], F32)
         products = {}
 
         def multiply(c):
             heads = widths[c] // HEAD
-            product = work.tile([SEQ, 3, heads * PAIRS], F32)
-            for bank, row in banks[c]:
-                rows = bank.shape[1] // (heads * PAIRS)
-                nc.vector.tensor_tensor(
-                    out=product[:, row : row + rows, :].rearrange("p j (h i) -> p j h i", h=heads),
-                    in0=bank.rearrange("p (j h i) -> p j h i", j=rows, h=heads),
-                    in1=factors[:, row : row + rows, :].unsqueeze(2).to_broadcast([SEQ, rows, heads, PAIRS]),
-                    op=MULT,
-                )
-            products[c] = product
+            lanes = work.tile([SEQ, heads * PAIRS, 2], F32)
+            nc.vector.tensor_tensor(
+                out=lanes[:].rearrange("p (h i) e -> p h i e", h=heads),
+                in0=banks[c].rearrange("p (e h i) -> p h i e", e=2, h=heads)[:, :, :, ::-1],
+                in1=crossed[:].unsqueeze(1).to_broadcast([SEQ, heads, PAIRS, 2]),
+                op=MULT,
+            )
+            shared = work.tile([SEQ, heads * PAIRS], F32)
+            nc.vector.tensor_tensor(
+                out=shared[:].rearrange("p (h i) -> p h i", h=heads),
+                in0=sums[c].rearrange("p (h i) -> p h i", h=heads),
+                in1=cos_f32[:].unsqueeze(1).to_broadcast([SEQ, heads, PAIRS]),
+                op=MULT,
+            )
+            products[c] = (lanes, shared)
 
         def store(c, result, first, heads):
             nc.sync.dma_start(
@@ -176,11 +182,12 @@ def tile_gqa_pa_s_kernel(tc, x, cos, sin, Wq, Wkv, out_0, out_1, out_2):
             )
 
         def add_and_store(engine, c, result, first, heads):
+            lanes, shared = products[c]
             pairs = slice(first * PAIRS, (first + heads) * PAIRS)
             engine.tensor_tensor(
                 out=result[:].rearrange("p (n e) -> p n e", e=2),
-                in0=products[c][:, 2, pairs].unsqueeze(2).to_broadcast([SEQ, heads * PAIRS, 2]),
-                in1=products[c][:, 0:2, pairs].rearrange("p e n -> p n e")[:, :, ::-1],
+                in0=shared[:, pairs].unsqueeze(2).to_broadcast([SEQ, heads * PAIRS, 2]),
+                in1=lanes[:, pairs, :],
                 op=ADD,
             )
             store(c, result, first, heads)
@@ -207,10 +214,10 @@ def tile_gqa_pa_s_kernel(tc, x, cos, sin, Wq, Wkv, out_0, out_1, out_2):
             out=x_grouped[:].bitcast(F32).rearrange("p (s u) -> p s u", u=2),
             in_=x_t[:].rearrange("p u s -> p s u"),
         )
-        nc.scalar.copy(out=factors[:, 2, :], in_=cos_sb[:])
-        nc.vector.tensor_tensor(out=factors[:, 0, :], in0=sin_sb[:], in1=cos_sb[:], op=SUB)
+        nc.scalar.copy(out=cos_f32[:], in_=cos_sb[:])
+        nc.vector.tensor_tensor(out=crossed[:, :, 1], in0=sin_sb[:], in1=cos_sb[:], op=SUB)
         nc.vector.scalar_tensor_tensor(
-            out=factors[:, 1, :], in0=cos_sb[:], scalar=-1.0, in1=sin_sb[:], op0=MULT, op1=SUB
+            out=crossed[:, :, 0], in0=cos_sb[:], scalar=-1.0, in1=sin_sb[:], op0=MULT, op1=SUB
         )
         quantise(0)
         nc.vector.quantize_mx(out=x_codes[:].bitcast(FP8X4), scales=x_scales[:], in_=x_grouped[:])
@@ -244,7 +251,7 @@ def tile_gqa_pa_s_kernel(tc, x, cos, sin, Wq, Wkv, out_0, out_1, out_2):
         combine_vector(3, GPSIMD_HEADS[3])
 
         values = work.tile([SEQ, CHUNK], F32)
-        nc.scalar.copy(out=values[:], in_=banks[VALUES][0][0])
+        nc.scalar.copy(out=values[:], in_=banks[VALUES])
         store(VALUES, values, 0, GROUP)
 
         quantise(6)

@@ -26,9 +26,9 @@ RUN = 8
 VALUES = Q_HEADS // GROUP
 KEYS = VALUES + 1
 
-VECTOR_COLS = (320, 320, 0, 320, 0, 0, 0)
+VECTOR_COLS = (320, 320, 0, 352, 0, 0, 0)
 GPSIMD_COLS = (0, 0, 160, 0, 0, 0, 0)
-GPSIMD_HEADS = (4, 3, 3, 2)
+GPSIMD_HEADS = (3, 3, 2, 2)
 
 FLOPS = 2 * SEQ * DIM * (Q_HEADS + 2 * KV_HEADS) * HEAD
 
@@ -153,6 +153,10 @@ def tile_gqa_pa_s_kernel(tc, x, cos, sin, Wq, Wkv, out_0, out_1, out_2):
             for e in range(2):
                 pass_mx(c, sums[c], e * (width // 2), (e + 1) * (width // 2), e == 0, e == 1)
 
+        def keep_clock(times):
+            for again in range(times):
+                nc.tensor.matmul(x_t[:, 0, :], lhsT=ident[:], rhs=ident[:], start=True, stop=True)
+
         crossed = const.tile([SEQ, PAIRS, 2], F32)
         cos_f32 = const.tile([SEQ, PAIRS], F32)
         products = {}
@@ -238,11 +242,14 @@ def tile_gqa_pa_s_kernel(tc, x, cos, sin, Wq, Wkv, out_0, out_1, out_2):
         combine_gpsimd(0, over=2)
         quantise(3)
         project(3)
+        keep_clock(2)
         multiply(1)
+        combine_vector(0, GPSIMD_HEADS[0])
         combine_gpsimd(1)
         multiply(2)
         quantise(4)
         project(4)
+        keep_clock(1)
         multiply(3)
         combine_vector(2, GPSIMD_HEADS[2])
         combine_gpsimd(2)

@@ -26,9 +26,9 @@ RUN = 8
 VALUES = Q_HEADS // GROUP
 KEYS = VALUES + 1
 
-VECTOR_COLS = (320, 320, 0, 352, 0, 0, 0)
+VECTOR_COLS = (320, 320, 0, 320, 0, 0, 0)
 GPSIMD_COLS = (0, 0, 160, 0, 0, 0, 0)
-GPSIMD_HEADS = (3, 3, 2, 2)
+GPSIMD_HEADS = (3, 2, 2, 2)
 
 FLOPS = 2 * SEQ * DIM * (Q_HEADS + 2 * KV_HEADS) * HEAD
 
@@ -239,23 +239,24 @@ def tile_gqa_pa_s_kernel(tc, x, cos, sin, Wq, Wkv, out_0, out_1, out_2):
             regroup_scalar(later)
         quantise(2)
         project(2)
+        combine_vector(0, GPSIMD_HEADS[0])
         combine_gpsimd(0, over=2)
         quantise(3)
         project(3)
         keep_clock(2)
         multiply(1)
-        combine_vector(0, GPSIMD_HEADS[0])
         combine_gpsimd(1)
         multiply(2)
+        combine_gpsimd(2)
+        multiply(3)
         quantise(4)
         project(4)
         keep_clock(1)
-        multiply(3)
         combine_vector(2, GPSIMD_HEADS[2])
-        combine_gpsimd(2)
+        combine_vector(3, GPSIMD_HEADS[3])
         quantise(5)
         project(5)
-        combine_vector(3, GPSIMD_HEADS[3])
+        combine_vector(1, GPSIMD_HEADS[1])
 
         values = work.tile([SEQ, CHUNK], F32)
         nc.scalar.copy(out=values[:], in_=banks[VALUES])
@@ -263,7 +264,6 @@ def tile_gqa_pa_s_kernel(tc, x, cos, sin, Wq, Wkv, out_0, out_1, out_2):
 
         quantise(6)
         project(6)
-        combine_vector(1, GPSIMD_HEADS[1])
         combine_gpsimd(3, over=6)
         multiply(5)
         multiply(6)

from contextlib import ExitStack

import concourse.mybir as mybir
from concourse.masks import make_identity

BF16 = mybir.dt.bfloat16
F32 = mybir.dt.float32
U32 = mybir.dt.uint32
U8 = mybir.dt.uint8
FP8X4 = mybir.dt.float8_e4m3fn_x4
MULT = mybir.AluOpType.mult
ADD = mybir.AluOpType.add
SUB = mybir.AluOpType.subtract

P = 128
PACK = 4
SEQ = 128
DIM = P * PACK
HEAD = 128
PAIRS = HEAD // 2
Q_HEADS = 16
KV_HEADS = 4
GROUP = 4
CHUNK = GROUP * HEAD
RUN = 8
VALUES = Q_HEADS // GROUP
KEYS = VALUES + 1

VECTOR_COLS = (320, 320, 0, 320, 0, 0, 0)
GPSIMD_COLS = (0, 0, 160, 0, 0, 0, 0)
GPSIMD_HEADS = (3, 2, 2, 2)

FLOPS = 2 * SEQ * DIM * (Q_HEADS + 2 * KV_HEADS) * HEAD


def tile_gqa_pa_s_kernel(tc, x, cos, sin, Wq, Wkv, out_0, out_1, out_2):
    nc = tc.nc

    half = GROUP // 2
    chunks = [out_0[0, g * GROUP : (g + 1) * GROUP] for g in range(VALUES)]
    chunks.append(out_2[0])
    chunks += [out_1[0, g * half : (g + 1) * half] for g in range(2)]
    n_chunks = len(chunks)
    widths = [heads_out.shape[0] * HEAD for heads_out in chunks]
    loads = [Wq[:, g * CHUNK : (g + 1) * CHUNK] for g in range(VALUES)]
    loads += [Wkv[:, CHUNK : 2 * CHUNK], Wkv[:, 0:CHUNK]]

    with ExitStack() as ctx:
        const = ctx.enter_context(tc.tile_pool(name="const", bufs=1))
        weights = ctx.enter_context(tc.tile_pool(name="weights", bufs=n_chunks))
        work = ctx.enter_context(tc.tile_pool(name="work", bufs=n_chunks))
        overlay = ctx.enter_context(tc.tile_pool(name="overlay", bufs=1))
        psum_x = ctx.enter_context(tc.psum_pool(name="psum_x", bufs=1))
        psum = ctx.enter_context(tc.psum_pool(name="psum", bufs=4))
        psum_sums = ctx.enter_context(tc.psum_pool(name="psum_sums", bufs=3))
        ctx.enter_context(tc.manual_schedule())

        raws = []
        for g in range(len(loads)):
            raw = weights.tile([P, PACK, CHUNK], BF16)
            nc.sync.dma_start(out=raw[:], in_=loads[g].rearrange("(p t) w -> p t w", t=PACK))
            raws.append(raw)
            if g == 0:
                x_sb = const.tile([SEQ, DIM], BF16)
                nc.sync.dma_start(out=x_sb[:], in_=x[0])
                cos_sb = const.tile([SEQ, PAIRS], BF16)
                nc.sync.dma_start(out=cos_sb[:], in_=cos)
                sin_sb = const.tile([SEQ, PAIRS], BF16)
                nc.sync.dma_start(out=sin_sb[:], in_=sin)
        sources = [raws[c][:] for c in range(KEYS)]
        for g in range(2):
            sources.append(raws[KEYS][:, :, g * half * HEAD : (g + 1) * half * HEAD])

        warm = const.tile([P, 2], F32)
        nc.vector.memset(warm[:], 0.0)
        nc.scalar.copy(out=warm[:, 1:2], in_=warm[:, 0:1])

        ident = const.tile([P, P], F32)
        make_identity(nc, ident[:])
        x_words = x_sb[:].bitcast(F32).rearrange("s (p u) -> s u p", u=2)
        x_t = psum_x.tile([P, 2, SEQ], F32)
        for u in range(2):
            nc.tensor.transpose(x_t[:, u, :], x_words[:, u, :], ident[:])

        places = [sum(widths[:c]) * PACK * 2 for c in range(n_chunks)]
        groupeds = []
        for c in range(n_chunks):
            groupeds.append(
                overlay.tile([P, widths[c], PACK], BF16, name="grouped%d" % c, offset=places[c], align_bytes=64)
            )

        def views(c, lo, hi):
            if c == VALUES:
                out = groupeds[c][:, lo:hi, :].rearrange("p (b i) t -> p b t i", i=RUN)
                return out, sources[c][:, :, lo:hi].rearrange("p t (b i) -> p b t i", i=RUN)
            out = groupeds[c][:].rearrange("p (e b n) t -> p b t n e", e=2, n=RUN // 2)
            in_ = sources[c][:].rearrange("p t (b n e) -> p b t n e", e=2, n=RUN // 2)
            blocks = slice(lo // RUN, hi // RUN)
            return out[:, blocks], in_[:, blocks]

        def regroup_vector(c):
            out, in_ = views(c, 0, VECTOR_COLS[c])
            nc.vector.tensor_copy(out=out, in_=in_)

        def regroup_gpsimd(c):
            pairs = slice(VECTOR_COLS[c] // 2, (VECTOR_COLS[c] + GPSIMD_COLS[c]) // 2)
            out = groupeds[c][:].rearrange("p (e n) t -> p e n t", e=2)[:, :, pairs]
            in_ = sources[c][:].rearrange("p t (n e) -> p e n t", e=2)[:, :, pairs]
            nc.gpsimd.tensor_scalar(out=out, in0=in_, scalar1=1.0, scalar2=0.0, op0=MULT, op1=ADD)

        def regroup_scalar(c):
            out, in_ = views(c, VECTOR_COLS[c] + GPSIMD_COLS[c], widths[c])
            nc.scalar.copy(out=out, in_=in_)

        x_codes = const.tile([P, SEQ], U32, align_bytes=64)
        x_scales = const.tile([P, SEQ], U8, align_bytes=64)
        quantised = {}

        def quantise(c):
            codes = weights.tile([P, widths[c]], U32, align_bytes=64)
            scales = weights.tile([P, widths[c]], U8, align_bytes=64)
            nc.vector.quantize_mx(
                out=codes[:].bitcast(FP8X4),
                scales=scales[:],
                in_=groupeds[c][:].rearrange("p w t -> p (w t)"),
            )
            quantised[c] = (codes, scales)

        def pass_mx(c, out, lo, hi, start, stop):
            codes, scales = quantised[c]
            nc.tensor.matmul_mx(
                out=out,
                lhsT=x_codes[:].bitcast(FP8X4),
                lhsT_scale=x_scales[:],
                rhs=codes[:, lo:hi].bitcast(FP8X4),
                rhs_scale=scales[:, lo:hi],
                start=start,
                stop=stop,
            )

        banks = {}
        sums = {}

        def project(c):
            width = widths[c]
            acc = psum.tile([SEQ, CHUNK], F32)
            pass_mx(c, acc[:, 0:width], 0, width, True, True)
            banks[c] = acc[:, 0:width]
            if c == VALUES:
                return
            sums_bank = psum_sums.tile([SEQ, CHUNK], F32)
            sums[c] = sums_bank[:, 0 : width // 2]
            for e in range(2):
                pass_mx(c, sums[c], e * (width // 2), (e + 1) * (width // 2), e == 0, e == 1)

        def keep_clock(times):
            for again in range(times):
                nc.tensor.matmul(x_t[:, 0, :], lhsT=ident[:], rhs=ident[:], start=True, stop=True)

        crossed = const.tile([SEQ, PAIRS, 2], F32)
        cos_f32 = const.tile([SEQ, PAIRS], F32)
        products = {}

        def multiply(c):
            heads = widths[c] // HEAD
            lanes = work.tile([SEQ, heads * PAIRS, 2], F32)
            nc.vector.tensor_tensor(
                out=lanes[:].rearrange("p (h i) e -> p h i e", h=heads),
                in0=banks[c].rearrange("p (e h i) -> p h i e", e=2, h=heads)[:, :, :, ::-1],
                in1=crossed[:].unsqueeze(1).to_broadcast([SEQ, heads, PAIRS, 2]),
                op=MULT,
            )
            shared = work.tile([SEQ, heads * PAIRS], F32)
            nc.vector.tensor_tensor(
                out=shared[:].rearrange("p (h i) -> p h i", h=heads),
                in0=sums[c].rearrange("p (h i) -> p h i", h=heads),
                in1=cos_f32[:].unsqueeze(1).to_broadcast([SEQ, heads, PAIRS]),
                op=MULT,
            )
            products[c] = (lanes, shared)

        def store(c, result, first, heads):
            nc.sync.dma_start(
                out=chunks[c][first : first + heads].rearrange("h s d -> s h d"),
                in_=result[:].rearrange("p (h d) -> p h d", h=heads),
            )

        def add_and_store(engine, c, result, first, heads):
            lanes, shared = products[c]
            pairs = slice(first * PAIRS, (first + heads) * PAIRS)
            engine.tensor_tensor(
                out=result[:].rearrange("p (n e) -> p n e", e=2),
                in0=shared[:, pairs].unsqueeze(2).to_broadcast([SEQ, heads * PAIRS, 2]),
                in1=lanes[:, pairs, :],
                op=ADD,
            )
            store(c, result, first, heads)

        def combine_vector(c, first):
            heads = widths[c] // HEAD - first
            result_v = work.tile([SEQ, heads * HEAD], F32)
            add_and_store(nc.vector, c, result_v, first, heads)

        def combine_gpsimd(c, over=None):
            heads = GPSIMD_HEADS[c]
            if over is None:
                result_g = work.tile([SEQ, heads * HEAD], F32)
            else:
                result_g = overlay.tile(
                    [SEQ, heads * HEAD], F32, name="result%d" % c, offset=places[over], align_bytes=64
                )
            add_and_store(nc.gpsimd, c, result_g, 0, heads)

        regroup_vector(0)
        regroup_scalar(0)
        x_grouped = const.tile([P, SEQ * PACK], BF16, align_bytes=64)
        nc.scalar.copy(
            out=x_grouped[:].bitcast(F32).rearrange("p (s u) -> p s u", u=2),
            in_=x_t[:].rearrange("p u s -> p s u"),
        )
        nc.scalar.copy(out=cos_f32[:], in_=cos_sb[:])
        nc.vector.tensor_tensor(out=crossed[:, :, 1], in0=sin_sb[:], in1=cos_sb[:], op=SUB)
        nc.vector.scalar_tensor_tensor(
            out=crossed[:, :, 0], in0=cos_sb[:], scalar=-1.0, in1=sin_sb[:], op0=MULT, op1=SUB
        )
        quantise(0)
        nc.vector.quantize_mx(out=x_codes[:].bitcast(FP8X4), scales=x_scales[:], in_=x_grouped[:])
        project(0)
        regroup_vector(1)
        regroup_scalar(1)
        quantise(1)
        project(1)
        regroup_gpsimd(2)
        regroup_scalar(2)

        multiply(0)
        regroup_vector(3)
        for later in range(3, n_chunks):
            regroup_scalar(later)
        quantise(2)
        project(2)
        combine_vector(0, GPSIMD_HEADS[0])
        combine_gpsimd(0, over=2)
        quantise(3)
        project(3)
        keep_clock(2)
        multiply(1)
        combine_gpsimd(1)
        multiply(2)
        combine_gpsimd(2)
        multiply(3)
        quantise(4)
        project(4)
        keep_clock(1)
        combine_vector(2, GPSIMD_HEADS[2])
        combine_vector(3, GPSIMD_HEADS[3])
        quantise(5)
        project(5)
        combine_vector(1, GPSIMD_HEADS[1])

        values = work.tile([SEQ, CHUNK], F32)
        nc.scalar.copy(out=values[:], in_=banks[VALUES])
        store(VALUES, values, 0, GROUP)

        quantise(6)
        project(6)
        combine_gpsimd(3, over=6)
        multiply(5)
        multiply(6)
        combine_vector(5, 0)
        combine_vector(6, 0)
